import numpy as np
import ml_dtypes


def mxq(x, axis, fmt="e4m3"):
    dtype, down = {"e4m3": (ml_dtypes.float8_e4m3fn, 7), "e5m2": (ml_dtypes.float8_e5m2, 14)}[fmt]
    v = np.moveaxis(np.asarray(x, np.float32).astype(ml_dtypes.bfloat16).astype(np.float64), axis, -1)
    blocks = v.reshape(v.shape[:-1] + (-1, 32))
    amax = np.abs(blocks).max(-1, keepdims=True)
    byte = np.maximum(np.where(amax > 0, np.frexp(amax)[1] - 1 + 127, 0) - down, 1)
    scale = np.exp2(byte - 127.0)
    codes = (blocks / scale).astype(np.float32).astype(dtype).astype(np.float64)
    return np.moveaxis((codes * scale).reshape(v.shape), -1, axis)


WIDE = False


def mx_kscale(k):
    if not WIDE:
        return np.ones(k)
    levels = np.array([10, -10, 5, -5, 0])
    a = np.random.permutation(np.resize(levels, k // 512 * 4)).reshape(k // 512, 4)
    idx = np.arange(k)
    return np.exp2(a[idx // 512, idx % 128 // 32])


BF16 = ml_dtypes.bfloat16


def bf(x):
    return np.asarray(x, np.float32).astype(BF16)


def f64(x):
    return np.asarray(x).astype(np.float64)


B, S, D, H, HD, C = 1, 512, 1024, 8, 128, 2
DM = HD * C
DIFF = C - 1
EPS = 1e-9


def softmax(z):
    e = np.exp(z - z.max(-1, keepdims=True))
    return e / e.sum(-1, keepdims=True)


def setup_inputs():
    s = mx_kscale(D)
    a = np.sqrt(0.085 / (H * np.sqrt(HD)))
    return {"q_rot": bf(np.random.standard_normal((B, S, H, DM))),
            "k_rot": bf(np.random.standard_normal((B, S, H, DM))),
            "h_norm": bf(np.random.standard_normal((B, S, D)) * s),
            "wv": bf(np.random.standard_normal((H * HD, D)) / np.sqrt(D) / s[None, :]),
            "head_norm_w": bf(1.0 + 0.1 * np.random.standard_normal(HD)),
            "q1": bf(np.random.standard_normal((H, HD, DIFF)) * a),
            "q2": bf(np.random.standard_normal((H, HD, DIFF)) * a),
            "k1": bf(np.random.standard_normal((H, HD, DIFF)) * a),
            "k2": bf(np.random.standard_normal((H, HD, DIFF)) * a),
            "lam_init": bf(0.5 / H + 0.08 / np.sqrt(H) * np.random.standard_normal(H))}


def reference(q_rot, k_rot, h_norm, wv, head_norm_w, q1, q2, k1, k2, lam_init):
    lam = f64(lam_init)
    v = (mxq(f64(h_norm), 2, "e4m3") @ mxq(f64(wv), 1, "e4m3").T).reshape(B, S, H, HD)
    qc = f64(q_rot).reshape(B, S, H, C, HD).transpose(0, 2, 3, 1, 4)
    kc = f64(k_rot).reshape(B, S, H, C, HD).transpose(0, 2, 3, 4, 1)
    energy = qc @ kc
    mask = np.triu(np.ones((S, S), dtype=bool), 1)
    energy = np.where(mask, -np.inf, energy)
    scores = softmax(energy / np.sqrt(HD))
    base = np.exp(np.sum(f64(q1) * f64(k1), axis=-2)) - np.exp(np.sum(f64(q2) * f64(k2), axis=-2))
    scale = -(H * base[:, 0] + np.sum(lam))
    sc = scores[:, :, 0] + scores[:, :, 1] * scale[None, :, None, None]
    vv = v.transpose(0, 2, 1, 3)
    att = (mxq(sc, 3, "e4m3") @ mxq(vv, 2, "e4m3")).transpose(0, 2, 1, 3)
    att = att / np.sqrt(np.mean(att * att, axis=-1, keepdims=True) + EPS) * f64(head_norm_w)
    return att * (1.0 - lam[None, None, :, None])

@@ -1,0 +1,359 @@
+from contextlib import ExitStack
+
+import concourse.mybir as mybir
+from concourse.masks import make_identity
+
+FP8X4 = mybir.dt.float8_e4m3fn_x4
+BF16 = mybir.dt.bfloat16
+F32 = mybir.dt.float32
+U32 = mybir.dt.uint32
+U8 = mybir.dt.uint8
+ALU = mybir.AluOpType
+ACT = mybir.ActivationFunctionType
+AX = mybir.AxisListType
+
+P = 128
+S = 512
+D = 1024
+H = 8
+HD = 128
+C = 2
+ROW_TILES = S // P
+PACK = 4
+D_PASSES = D // (PACK * P)
+QUAD = 4
+PAIR = 2
+SM_SCALE = 1.0 / (HD ** 0.5)
+EPS = 1e-9
+MASKED = -1.0e30
+
+FLOPS = 2 * S * D * H * HD + 2 * H * C * S * S * HD + 2 * H * S * S * HD
+
+
+def tile_attention_pb_kernel(
+    tc, q_rot, k_rot, h_norm, wv, head_norm_w, q1, q2, k1, k2, lam_init, out
+):
+    nc = tc.nc
+    with ExitStack() as ctx:
+        consts = ctx.enter_context(tc.tile_pool(name="consts", bufs=1))
+        loads = ctx.enter_context(tc.tile_pool(name="loads", bufs=1))
+        keep = ctx.enter_context(tc.tile_pool(name="keep", bufs=1))
+        work = ctx.enter_context(tc.tile_pool(name="work", bufs=2))
+        small = ctx.enter_context(tc.tile_pool(name="small", bufs=6))
+        psum_e = ctx.enter_context(tc.psum_pool(name="psum_e", bufs=5))
+        psum_t = ctx.enter_context(tc.psum_pool(name="psum_t", bufs=2))
+        psum_att = ctx.enter_context(tc.psum_pool(name="psum_att", bufs=1))
+
+        qk_vec = consts.tile([H, 4, HD], BF16, name="qk_vec")
+        for n, vec in enumerate((q1, q2, k1, k2)):
+            nc.sync.dma_start(out=qk_vec[:, n, :], in_=vec.rearrange("h d o -> h (d o)"))
+        lam_all = consts.tile([P, H], BF16, name="lam_all")
+        nc.sync.dma_start(out=lam_all[:], in_=lam_init.partition_broadcast(P))
+
+        q_rows = q_rot.rearrange("b s h m -> (b s) (h m)")
+        k_rows = k_rot.rearrange("b s h m -> (b s) (h m)")
+        q_sb = [loads.tile([P, H * C * HD], BF16, name="q_sb%d" % it) for it in range(ROW_TILES)]
+        k_sb = [loads.tile([P, H * C * HD], BF16, name="k_sb%d" % it) for it in range(ROW_TILES)]
+        h_sb = loads.tile([P, ROW_TILES, D], BF16, name="h_sb")
+        w_sb = loads.tile([P, H, D], BF16, name="w_sb")
+        w_all = consts.tile([P, HD], BF16, name="w_all")
+
+        def load_qk(it, pieces):
+            rows = slice(it * P, (it + 1) * P)
+            width = H * C * HD // pieces
+            for piece in range(pieces):
+                cols = slice(piece * width, (piece + 1) * width)
+                nc.sync.dma_start(out=q_sb[it][:, cols], in_=q_rows[rows, cols])
+                nc.sync.dma_start(out=k_sb[it][:, cols], in_=k_rows[rows, cols])
+
+        load_qk(0, pieces=2)
+        nc.sync.dma_start(out=w_all[:], in_=head_norm_w.partition_broadcast(P))
+        nc.sync.dma_start(
+            out=h_sb[:].rearrange("p (u e) k -> p u (e k)", u=2),
+            in_=h_norm.rearrange("b s k -> (b s) k").rearrange("(u p e) k -> p u (e k)", u=2, e=2),
+        )
+        w_tiles = wv.rearrange("(o p) k -> p o k", p=P)
+        for half in range(H // QUAD):
+            heads = slice(half * QUAD, (half + 1) * QUAD)
+            nc.sync.dma_start(out=w_sb[:, heads, :], in_=w_tiles[:, heads, :])
+        for it in range(1, ROW_TILES):
+            load_qk(it, pieces=1)
+
+        ident_bf = consts.tile([P, P], BF16, name="ident_bf")
+        nc.vector.memset(ident_bf[:], 0.0)
+        make_identity(nc, ident_bf[:], nomemset=True)
+        ident_f32 = consts.tile([P, P], F32, name="ident_f32")
+        nc.vector.memset(ident_f32[:], 0.0)
+        make_identity(nc, ident_f32[:], nomemset=True)
+        mask_f32 = consts.tile([P, P], F32, name="mask_f32")
+        nc.vector.memset(mask_f32[:], 0.0)
+        nc.gpsimd.affine_select(
+            out=mask_f32[:],
+            in_=mask_f32[:],
+            compare_op=ALU.is_ge,
+            fill=MASKED,
+            base=0,
+            pattern=[[-1, P]],
+            channel_multiplier=1,
+        )
+        mask_bf = consts.tile([P, P], BF16, name="mask_bf")
+        nc.vector.tensor_copy(out=mask_bf[:], in_=mask_f32[:])
+        neg_half = consts.tile([P, PAIR], F32, name="neg_half")
+        nc.vector.memset(neg_half[:], -0.5)
+        warm = consts.tile([P, 1], F32, name="warm")
+        nc.scalar.activation(out=warm[:], in_=neg_half[:, 0:1], func=ACT.Exp)
+
+        sc_sb = [keep.tile([P, S], BF16, name="sc_sb%d" % h) for h in range(H)]
+        for h in range(H):
+            nc.vector.memset(sc_sb[h][:], 0.0)
+
+        prod = consts.tile([H, 2, HD], F32, name="prod")
+        nc.vector.tensor_tensor(out=prod[:], in0=qk_vec[:, 0:2, :], in1=qk_vec[:, 2:4, :], op=ALU.mult)
+        dots = consts.tile([H, 2], F32, name="dots")
+        nc.vector.reduce_sum(out=dots[:], in_=prod[:], axis=AX.X)
+        exps = consts.tile([H, 2], F32, name="exps")
+        nc.scalar.activation(out=exps[:], in_=dots[:], func=ACT.Exp)
+        base = consts.tile([P, 1], F32, name="base")
+        nc.vector.memset(base[:], 0.0)
+        nc.vector.tensor_sub(out=base[0:H, :], in0=exps[:, 0:1], in1=exps[:, 1:2])
+        base_all = psum_att.tile([P, P], F32, name="base_all", tag="att")
+        nc.tensor.matmul(
+            base_all[:], lhsT=base[:, 0:1].to_broadcast([P, P]), rhs=ident_f32[:], start=True, stop=True
+        )
+        lam_sum = consts.tile([P, 1], F32, name="lam_sum")
+        nc.vector.reduce_sum(out=lam_sum[:], in_=lam_all[:], axis=AX.X)
+        scale_all = consts.tile([P, H], F32, name="scale_all")
+        nc.vector.tensor_scalar(
+            out=scale_all[:],
+            in0=base_all[:, 0:H],
+            scalar1=-float(H),
+            scalar2=lam_sum[:, 0:1],
+            op0=ALU.mult,
+            op1=ALU.subtract,
+        )
+        one_minus_lam = consts.tile([P, H], F32, name="one_minus_lam")
+        nc.gpsimd.tensor_scalar(
+            out=one_minus_lam[:], in0=lam_all[:], scalar1=-1.0, scalar2=1.0, op0=ALU.mult, op1=ALU.add
+        )
+        gain = consts.tile([P, H, HD], F32, name="gain")
+        for h in range(H):
+            nc.gpsimd.tensor_scalar(
+                out=gain[:, h, :],
+                in0=w_all[:],
+                scalar1=one_minus_lam[:, h : h + 1],
+                scalar2=0.0,
+                op0=ALU.mult,
+                op1=ALU.add,
+            )
+
+        qT = keep.tile([P, H * C, S], BF16, name="qT")
+        kT = keep.tile([P, H * C, S], BF16, name="kT")
+
+        def transpose_qk(it, piece):
+            cols = slice(it * P, (it + 1) * P)
+            rows_sb, flipped = ((q_sb[it], qT), (k_sb[it], kT))[piece % 2]
+            first = (piece // 2) * QUAD * C
+            bank = psum_t.tile([P, QUAD * C, P], BF16, name="qk_bank", tag="t")
+            for m in range(QUAD * C):
+                hc = first + m
+                nc.tensor.transpose(bank[:, m, :], rows_sb[:, hc * HD : (hc + 1) * HD], ident_bf[:])
+            nc.scalar.copy(out=flipped[:, first : first + QUAD * C, cols], in_=bank[:])
+
+        def word_transposes(bank, pair_words):
+            for r in range(2):
+                for u in range(2):
+                    nc.tensor.transpose(bank[:, r, u, :], pair_words[r][:, u * P : (u + 1) * P], ident_f32[:])
+
+        def quantise_512_rows(rows_words, codes, scales):
+            grouped = work.tile([P, D_PASSES, QUAD * P, PACK], BF16, name="grouped", align_bytes=64)
+            grouped_words = grouped[:].bitcast(F32)
+            for g in range(D_PASSES):
+                for pair in range(2):
+                    bank = psum_e.tile([P, 2, 2, P], F32, name="kl_bank", tag="e")
+                    word_transposes(
+                        bank,
+                        [rows_words[:, 2 * pair + r, g * 2 * P : (g + 1) * 2 * P] for r in range(2)],
+                    )
+                    regrouped = grouped_words[:, g, pair * 2 * P : (pair + 1) * 2 * P, :].rearrange(
+                        "p (r c) u -> p r c u", r=2
+                    )
+                    if pair == 0:
+                        nc.vector.tensor_copy(out=regrouped, in_=bank[:].rearrange("p r u c -> p r c u"))
+                    else:
+                        nc.scalar.copy(out=regrouped, in_=bank[:].rearrange("p r u c -> p r c u"))
+                nc.vector.quantize_mx(
+                    out=codes[:, g, :].bitcast(FP8X4),
+                    scales=scales[:, g, :],
+                    in_=grouped[:, g, :, :].rearrange("p c t -> p (c t)"),
+                )
+
+        h_codes = keep.tile([P, D_PASSES, S], U32, name="h_codes", align_bytes=64)
+        h_scales = keep.tile([P, D_PASSES, S], U8, name="h_scales", align_bytes=64)
+        w_codes = keep.tile([P, D_PASSES, H * HD], U32, name="w_codes", align_bytes=64)
+        w_scales = keep.tile([P, D_PASSES, H * HD], U8, name="w_scales", align_bytes=64)
+        v_grouped = keep.tile([P, H, HD, PACK], BF16, name="v_grouped", align_bytes=64)
+        v_codes = keep.tile([P, H * HD], U32, name="v_codes", align_bytes=64)
+        v_scales = keep.tile([P, H * HD], U8, name="v_scales", align_bytes=64)
+
+        def project_values(half):
+            for a in range(QUAD):
+                h = half * QUAD + a
+                d_cols = slice(h * HD, (h + 1) * HD)
+                v_bank = psum_e.tile([P, ROW_TILES, HD], F32, name="v_bank", tag="e")
+                for t in range(ROW_TILES):
+                    j_cols = slice(t * P, (t + 1) * P)
+                    for g in range(D_PASSES):
+                        nc.tensor.matmul_mx(
+                            out=v_bank[:, t, :],
+                            lhsT=h_codes[:, g, j_cols].bitcast(FP8X4),
+                            lhsT_scale=h_scales[:, g, j_cols],
+                            rhs=w_codes[:, g, d_cols].bitcast(FP8X4),
+                            rhs_scale=w_scales[:, g, d_cols],
+                            start=(g == 0),
+                            stop=(g == D_PASSES - 1),
+                        )
+                if h % 2 == 0:
+                    nc.vector.tensor_copy(out=v_grouped[:, h, :, :], in_=v_bank[:].rearrange("p t d -> p d t"))
+                else:
+                    nc.scalar.copy(out=v_grouped[:, h, :, :], in_=v_bank[:].rearrange("p t d -> p d t"))
+            cols = slice(half * QUAD * HD, (half + 1) * QUAD * HD)
+            nc.vector.quantize_mx(
+                out=v_codes[:, cols].bitcast(FP8X4),
+                scales=v_scales[:, cols],
+                in_=v_grouped[:, half * QUAD : (half + 1) * QUAD, :, :].rearrange("p a d t -> p (a d t)"),
+            )
+
+        def scores(it, h):
+            n = (it + 1) * P
+            rows = slice(it * P, n)
+            shift = small.tile([P, C], F32, name="shift")
+            sums = small.tile([P, C], F32, name="sums")
+            recip = small.tile([P, C], F32, name="recip")
+            energy = []
+            for c in range(C):
+                hc = h * C + c
+                e = psum_e.tile([P, S], F32, name="e", tag="e")
+                nc.tensor.matmul(e[:, :n], lhsT=qT[:, hc, rows], rhs=kT[:, hc, :n], start=True, stop=False)
+                nc.tensor.matmul(e[:, rows], lhsT=ident_bf[:], rhs=mask_bf[:], start=False, stop=True)
+                neg_scaled = work.tile([P, S], BF16, name="neg_scaled", bufs=3)
+                nc.vector.tensor_scalar(
+                    out=neg_scaled[:, :n],
+                    in0=e[:, :n],
+                    scalar1=-SM_SCALE,
+                    scalar2=None,
+                    op0=ALU.mult,
+                    op1=ALU.min,
+                    accum_out=shift[:, c : c + 1],
+                )
+                energy.append(e)
+            probs = []
+            for c in range(C):
+                p = work.tile([P, S], F32, name="p%d" % c, bufs=4)
+                nc.scalar.activation(
+                    out=p[:, :n],
+                    in_=energy[c][:, :n],
+                    func=ACT.Exp,
+                    bias=shift[:, c : c + 1],
+                    scale=SM_SCALE,
+                    accum_out=sums[:, c : c + 1],
+                )
+                probs.append(p)
+            nc.vector.reciprocal(out=recip[:], in_=sums[:])
+            nc.gpsimd.tensor_scalar(
+                out=probs[1][:, :n],
+                in0=probs[1][:, :n],
+                scalar1=recip[:, 1:2],
+                scalar2=scale_all[:, h : h + 1],
+                op0=ALU.mult,
+                op1=ALU.mult,
+            )
+            nc.vector.scalar_tensor_tensor(
+                out=sc_sb[h][:, :n],
+                in0=probs[0][:, :n],
+                scalar=recip[:, 0:1],
+                in1=probs[1][:, :n],
+                op0=ALU.mult,
+                op1=ALU.add,
+            )
+
+        def quantise_scores(pair):
+            bank = psum_t.tile([P, PAIR, 2, P], F32, name="sc_bank", tag="t")
+            word_transposes(bank, [sc_sb[pair * PAIR + r][:].bitcast(F32) for r in range(PAIR)])
+            sc_grouped = work.tile([P, PAIR, P, PACK], BF16, name="sc_grouped", align_bytes=64)
+            nc.scalar.copy(out=sc_grouped[:].bitcast(F32), in_=bank[:].rearrange("p r u c -> p r c u"))
+            sc_codes = work.tile([P, PAIR * P], U32, name="sc_codes", bufs=6, align_bytes=64)
+            sc_scales = work.tile([P, PAIR * P], U8, name="sc_scales", bufs=6, align_bytes=64)
+            nc.vector.quantize_mx(
+                out=sc_codes[:].bitcast(FP8X4),
+                scales=sc_scales[:],
+                in_=sc_grouped[:].rearrange("p r c t -> p (r c t)"),
+            )
+            return sc_codes, sc_scales
+
+        out_rows = out.rearrange("b s h d -> (b s) (h d)")
+
+        def attend(it, pair, sc_codes, sc_scales):
+            att = psum_att.tile([P, PAIR, HD], F32, name="att", tag="att")
+            for r in range(PAIR):
+                h = pair * PAIR + r
+                i_cols = slice(r * P, (r + 1) * P)
+                d_cols = slice(h * HD, (h + 1) * HD)
+                nc.tensor.matmul_mx(
+                    out=att[:, r, :],
+                    lhsT=sc_codes[:, i_cols].bitcast(FP8X4),
+                    lhsT_scale=sc_scales[:, i_cols],
+                    rhs=v_codes[:, d_cols].bitcast(FP8X4),
+                    rhs_scale=v_scales[:, d_cols],
+                    start=True,
+                    stop=True,
+                )
+            squares = work.tile([P, PAIR, HD], BF16, name="squares")
+            sum_sq = small.tile([P, PAIR], F32, name="sum_sq")
+            for r in range(PAIR):
+                nc.scalar.activation(
+                    out=squares[:, r, :], in_=att[:, r, :], func=ACT.Square, accum_out=sum_sq[:, r : r + 1]
+                )
+            mean_sq = small.tile([P, PAIR], F32, name="mean_sq")
+            nc.gpsimd.tensor_scalar(
+                out=mean_sq[:], in0=sum_sq[:], scalar1=1.0 / HD, scalar2=EPS, op0=ALU.mult, op1=ALU.add
+            )
+            rstd = small.tile([P, PAIR], F32, name="rstd")
+            nc.gpsimd.tensor_tensor(out=rstd[:], in0=mean_sq[:], in1=neg_half[:], op=ALU.pow)
+            normed = work.tile([P, PAIR, HD], F32, name="normed", bufs=3)
+            for r in range(PAIR):
+                nc.vector.scalar_tensor_tensor(
+                    out=normed[:, r, :],
+                    in0=att[:, r, :],
+                    scalar=rstd[:, r : r + 1],
+                    in1=gain[:, pair * PAIR + r, :],
+                    op0=ALU.mult,
+                    op1=ALU.mult,
+                )
+            nc.sync.dma_start(
+                out=out_rows[it * P : (it + 1) * P, pair * PAIR * HD : (pair + 1) * PAIR * HD],
+                in_=normed[:].rearrange("p r d -> p (r d)"),
+            )
+
+        def scores_of_two_heads(it, pair):
+            for r in range(PAIR):
+                scores(it, pair * PAIR + r)
+            if it + 1 < ROW_TILES:
+                transpose_qk(it + 1, pair)
+            return quantise_scores(pair)
+
+        for piece in range(4):
+            transpose_qk(0, piece)
+        tile0 = [scores_of_two_heads(0, pair) for pair in range(H // PAIR)]
+        quantise_512_rows(h_sb[:].bitcast(F32), h_codes, h_scales)
+        for half in range(H // QUAD):
+            heads = slice(half * QUAD, (half + 1) * QUAD)
+            cols = slice(half * QUAD * HD, (half + 1) * QUAD * HD)
+            quantise_512_rows(w_sb[:, heads, :].bitcast(F32), w_codes[:, :, cols], w_scales[:, :, cols])
+        for half in range(H // QUAD):
+            project_values(half)
+        for pair in range(H // PAIR):
+            attend(0, pair, tile0[pair][0], tile0[pair][1])
+        for it in range(1, ROW_TILES):
+            for pair in range(H // PAIR):
+                sc_codes, sc_scales = scores_of_two_heads(it, pair)
+                attend(it, pair, sc_codes, sc_scales)

@@ -259,7 +259,7 @@ def tile_attention_pb_kernel(
                 )
                 probs.append(p)
             nc.vector.reciprocal(out=recip[:], in_=sums[:])
-            nc.gpsimd.tensor_scalar(
+            nc.vector.tensor_scalar(
                 out=probs[1][:, :n],
                 in0=probs[1][:, :n],
                 scalar1=recip[:, 1:2],

@@ -23,9 +23,23 @@ PACK = 4
 D_PASSES = D // (PACK * P)
 QUAD = 4
 PAIR = 2
+UNITS = ROW_TILES * H
+PAIRS = UNITS // PAIR
 SM_SCALE = 1.0 / (HD ** 0.5)
 EPS = 1e-9
 MASKED = -1.0e30
+
+LAG_ENERGY = -1
+LAG_EXP = 0
+LAG_RESCALE = 1
+LAG_JOIN = 2
+LAG_FLIP = 4
+LAG_REGROUP = 5
+LAG_QUANTISE = 6
+LAG_MULTIPLY = 7
+LAG_SQUARES = 8
+LAG_RMS = 9
+LAG_FINISH = 10
 
 FLOPS = 2 * S * D * H * HD + 2 * H * C * S * S * HD + 2 * H * S * S * HD
 
@@ -40,51 +54,56 @@ def tile_attention_pb_kernel(
         keep = ctx.enter_context(tc.tile_pool(name="keep", bufs=1))
         work = ctx.enter_context(tc.tile_pool(name="work", bufs=2))
         small = ctx.enter_context(tc.tile_pool(name="small", bufs=6))
-        psum_e = ctx.enter_context(tc.psum_pool(name="psum_e", bufs=5))
+        psum_e = ctx.enter_context(tc.psum_pool(name="psum_e", bufs=4))
         psum_t = ctx.enter_context(tc.psum_pool(name="psum_t", bufs=2))
-        psum_att = ctx.enter_context(tc.psum_pool(name="psum_att", bufs=1))
+        psum_att = ctx.enter_context(tc.psum_pool(name="psum_att", bufs=2))
+        ctx.enter_context(tc.manual_schedule())
 
         qk_vec = consts.tile([H, 4, HD], BF16, name="qk_vec")
         for n, vec in enumerate((q1, q2, k1, k2)):
             nc.sync.dma_start(out=qk_vec[:, n, :], in_=vec.rearrange("h d o -> h (d o)"))
+
+        h_sb = loads.tile([P, ROW_TILES, D], BF16, name="h_sb")
+        h_halves = h_sb[:].rearrange("p (u e) k -> p u (e k)", u=2)
+        h_rows = h_norm.rearrange("b s k -> (b s) k").rearrange("(u p e) k -> p u (e k)", u=2, e=2)
+        for u in range(2):
+            nc.sync.dma_start(out=h_halves[:, u, :], in_=h_rows[:, u, :])
+
         lam_all = consts.tile([P, H], BF16, name="lam_all")
         nc.sync.dma_start(out=lam_all[:], in_=lam_init.partition_broadcast(P))
+        w_all = consts.tile([P, HD], BF16, name="w_all")
+        nc.sync.dma_start(out=w_all[:], in_=head_norm_w.partition_broadcast(P))
+
+        w_sb = loads.tile([P, H, D], BF16, name="w_sb")
+        w_tiles = wv.rearrange("(o p) k -> p o k", p=P)
+
+        def load_w(half):
+            for first in range(half * QUAD, (half + 1) * QUAD, PAIR):
+                heads = slice(first, first + PAIR)
+                nc.sync.dma_start(out=w_sb[:, heads, :], in_=w_tiles[:, heads, :])
 
         q_rows = q_rot.rearrange("b s h m -> (b s) (h m)")
         k_rows = k_rot.rearrange("b s h m -> (b s) (h m)")
         q_sb = [loads.tile([P, H * C * HD], BF16, name="q_sb%d" % it) for it in range(ROW_TILES)]
         k_sb = [loads.tile([P, H * C * HD], BF16, name="k_sb%d" % it) for it in range(ROW_TILES)]
-        h_sb = loads.tile([P, ROW_TILES, D], BF16, name="h_sb")
-        w_sb = loads.tile([P, H, D], BF16, name="w_sb")
-        w_all = consts.tile([P, HD], BF16, name="w_all")
 
-        def load_qk(it, pieces):
+        def load_qk(it):
             rows = slice(it * P, (it + 1) * P)
-            width = H * C * HD // pieces
-            for piece in range(pieces):
-                cols = slice(piece * width, (piece + 1) * width)
-                nc.sync.dma_start(out=q_sb[it][:, cols], in_=q_rows[rows, cols])
-                nc.sync.dma_start(out=k_sb[it][:, cols], in_=k_rows[rows, cols])
+            nc.sync.dma_start(out=q_sb[it][:], in_=q_rows[rows, :])
+            nc.sync.dma_start(out=k_sb[it][:], in_=k_rows[rows, :])
 
-        load_qk(0, pieces=2)
-        nc.sync.dma_start(out=w_all[:], in_=head_norm_w.partition_broadcast(P))
-        nc.sync.dma_start(
-            out=h_sb[:].rearrange("p (u e) k -> p u (e k)", u=2),
-            in_=h_norm.rearrange("b s k -> (b s) k").rearrange("(u p e) k -> p u (e k)", u=2, e=2),
-        )
-        w_tiles = wv.rearrange("(o p) k -> p o k", p=P)
-        for half in range(H // QUAD):
-            heads = slice(half * QUAD, (half + 1) * QUAD)
-            nc.sync.dma_start(out=w_sb[:, heads, :], in_=w_tiles[:, heads, :])
+        load_w(0)
+        load_qk(0)
+        load_w(1)
         for it in range(1, ROW_TILES):
-            load_qk(it, pieces=1)
+            load_qk(it)
 
-        ident_bf = consts.tile([P, P], BF16, name="ident_bf")
-        nc.vector.memset(ident_bf[:], 0.0)
-        make_identity(nc, ident_bf[:], nomemset=True)
         ident_f32 = consts.tile([P, P], F32, name="ident_f32")
         nc.vector.memset(ident_f32[:], 0.0)
         make_identity(nc, ident_f32[:], nomemset=True)
+        ident_bf = consts.tile([P, P], BF16, name="ident_bf")
+        nc.vector.memset(ident_bf[:], 0.0)
+        make_identity(nc, ident_bf[:], nomemset=True)
         mask_f32 = consts.tile([P, P], F32, name="mask_f32")
         nc.vector.memset(mask_f32[:], 0.0)
         nc.gpsimd.affine_select(
@@ -96,96 +115,102 @@ def tile_attention_pb_kernel(
             pattern=[[-1, P]],
             channel_multiplier=1,
         )
-        mask_bf = consts.tile([P, P], BF16, name="mask_bf")
-        nc.vector.tensor_copy(out=mask_bf[:], in_=mask_f32[:])
         neg_half = consts.tile([P, PAIR], F32, name="neg_half")
         nc.vector.memset(neg_half[:], -0.5)
         warm = consts.tile([P, 1], F32, name="warm")
         nc.scalar.activation(out=warm[:], in_=neg_half[:, 0:1], func=ACT.Exp)
-
         sc_sb = [keep.tile([P, S], BF16, name="sc_sb%d" % h) for h in range(H)]
         for h in range(H):
             nc.vector.memset(sc_sb[h][:], 0.0)
-
-        prod = consts.tile([H, 2, HD], F32, name="prod")
-        nc.vector.tensor_tensor(out=prod[:], in0=qk_vec[:, 0:2, :], in1=qk_vec[:, 2:4, :], op=ALU.mult)
-        dots = consts.tile([H, 2], F32, name="dots")
-        nc.vector.reduce_sum(out=dots[:], in_=prod[:], axis=AX.X)
-        exps = consts.tile([H, 2], F32, name="exps")
-        nc.scalar.activation(out=exps[:], in_=dots[:], func=ACT.Exp)
         base = consts.tile([P, 1], F32, name="base")
         nc.vector.memset(base[:], 0.0)
-        nc.vector.tensor_sub(out=base[0:H, :], in0=exps[:, 0:1], in1=exps[:, 1:2])
-        base_all = psum_att.tile([P, P], F32, name="base_all", tag="att")
-        nc.tensor.matmul(
-            base_all[:], lhsT=base[:, 0:1].to_broadcast([P, P]), rhs=ident_f32[:], start=True, stop=True
-        )
-        lam_sum = consts.tile([P, 1], F32, name="lam_sum")
-        nc.vector.reduce_sum(out=lam_sum[:], in_=lam_all[:], axis=AX.X)
+        mask_bf = consts.tile([P, P], BF16, name="mask_bf")
+        nc.vector.tensor_copy(out=mask_bf[:], in_=mask_f32[:])
+
         scale_all = consts.tile([P, H], F32, name="scale_all")
-        nc.vector.tensor_scalar(
-            out=scale_all[:],
-            in0=base_all[:, 0:H],
-            scalar1=-float(H),
-            scalar2=lam_sum[:, 0:1],
-            op0=ALU.mult,
-            op1=ALU.subtract,
-        )
-        one_minus_lam = consts.tile([P, H], F32, name="one_minus_lam")
-        nc.gpsimd.tensor_scalar(
-            out=one_minus_lam[:], in0=lam_all[:], scalar1=-1.0, scalar2=1.0, op0=ALU.mult, op1=ALU.add
-        )
         gain = consts.tile([P, H, HD], F32, name="gain")
-        for h in range(H):
-            nc.gpsimd.tensor_scalar(
-                out=gain[:, h, :],
-                in0=w_all[:],
-                scalar1=one_minus_lam[:, h : h + 1],
-                scalar2=0.0,
-                op0=ALU.mult,
-                op1=ALU.add,
+
+        def head_factors():
+            prod = consts.tile([H, 2, HD], F32, name="prod")
+            nc.vector.tensor_tensor(out=prod[:], in0=qk_vec[:, 0:2, :], in1=qk_vec[:, 2:4, :], op=ALU.mult)
+            dots = consts.tile([H, 2], F32, name="dots")
+            nc.vector.reduce_sum(out=dots[:], in_=prod[:], axis=AX.X)
+            exps = consts.tile([H, 2], F32, name="exps")
+            nc.scalar.activation(out=exps[:], in_=dots[:], func=ACT.Exp)
+            nc.vector.tensor_sub(out=base[0:H, :], in0=exps[:, 0:1], in1=exps[:, 1:2])
+            base_all = psum_att.tile([P, P], F32, name="base_all", tag="att")
+            nc.tensor.matmul(
+                base_all[:], lhsT=base[:, 0:1].to_broadcast([P, P]), rhs=ident_f32[:], start=True, stop=True
             )
+            lam_sum = consts.tile([P, 1], F32, name="lam_sum")
+            nc.vector.reduce_sum(out=lam_sum[:], in_=lam_all[:], axis=AX.X)
+            nc.vector.tensor_scalar(
+                out=scale_all[:],
+                in0=base_all[:, 0:H],
+                scalar1=-float(H),
+                scalar2=lam_sum[:, 0:1],
+                op0=ALU.mult,
+                op1=ALU.subtract,
+            )
+            one_minus_lam = consts.tile([P, H], F32, name="one_minus_lam")
+            nc.gpsimd.tensor_scalar(
+                out=one_minus_lam[:], in0=lam_all[:], scalar1=-1.0, scalar2=1.0, op0=ALU.mult, op1=ALU.add
+            )
+            for h in range(H):
+                nc.gpsimd.tensor_scalar(
+                    out=gain[:, h, :],
+                    in0=w_all[:],
+                    scalar1=one_minus_lam[:, h : h + 1],
+                    scalar2=0.0,
+                    op0=ALU.mult,
+                    op1=ALU.add,
+                )
 
         qT = keep.tile([P, H * C, S], BF16, name="qT")
         kT = keep.tile([P, H * C, S], BF16, name="kT")
 
-        def transpose_qk(it, piece):
-            cols = slice(it * P, (it + 1) * P)
-            rows_sb, flipped = ((q_sb[it], qT), (k_sb[it], kT))[piece % 2]
+        qk_banks = {}
+
+        def flip_qk(it, piece):
+            rows_sb = (q_sb[it], k_sb[it])[piece % 2]
             first = (piece // 2) * QUAD * C
             bank = psum_t.tile([P, QUAD * C, P], BF16, name="qk_bank", tag="t")
-            for m in range(QUAD * C):
-                hc = first + m
-                nc.tensor.transpose(bank[:, m, :], rows_sb[:, hc * HD : (hc + 1) * HD], ident_bf[:])
-            nc.scalar.copy(out=flipped[:, first : first + QUAD * C, cols], in_=bank[:])
+            for n in range(QUAD * C):
+                hc = first + n
+                nc.tensor.transpose(bank[:, n, :], rows_sb[:, hc * HD : (hc + 1) * HD], ident_bf[:])
+            qk_banks[(it, piece)] = bank
+
+        def keep_qk(it, piece, on_vector=False):
+            flipped = (qT, kT)[piece % 2]
+            first = (piece // 2) * QUAD * C
+            kept = flipped[:, first : first + QUAD * C, it * P : (it + 1) * P]
+            bank = qk_banks.pop((it, piece))
+            if on_vector:
+                nc.vector.tensor_copy(out=kept, in_=bank[:])
+            else:
+                nc.scalar.copy(out=kept, in_=bank[:])
 
         def word_transposes(bank, pair_words):
             for r in range(2):
                 for u in range(2):
                     nc.tensor.transpose(bank[:, r, u, :], pair_words[r][:, u * P : (u + 1) * P], ident_f32[:])
 
-        def quantise_512_rows(rows_words, codes, scales):
-            grouped = work.tile([P, D_PASSES, QUAD * P, PACK], BF16, name="grouped", align_bytes=64)
+        def regroup_512_rows(rows_words, g):
+            grouped = work.tile([P, QUAD * P, PACK], BF16, name="grouped", bufs=3, align_bytes=64)
             grouped_words = grouped[:].bitcast(F32)
-            for g in range(D_PASSES):
-                for pair in range(2):
-                    bank = psum_e.tile([P, 2, 2, P], F32, name="kl_bank", tag="e")
-                    word_transposes(
-                        bank,
-                        [rows_words[:, 2 * pair + r, g * 2 * P : (g + 1) * 2 * P] for r in range(2)],
-                    )
-                    regrouped = grouped_words[:, g, pair * 2 * P : (pair + 1) * 2 * P, :].rearrange(
-                        "p (r c) u -> p r c u", r=2
-                    )
-                    if pair == 0:
-                        nc.vector.tensor_copy(out=regrouped, in_=bank[:].rearrange("p r u c -> p r c u"))
-                    else:
-                        nc.scalar.copy(out=regrouped, in_=bank[:].rearrange("p r u c -> p r c u"))
-                nc.vector.quantize_mx(
-                    out=codes[:, g, :].bitcast(FP8X4),
-                    scales=scales[:, g, :],
-                    in_=grouped[:, g, :, :].rearrange("p c t -> p (c t)"),
+            for half in range(2):
+                bank = psum_e.tile([P, 2, 2, P], F32, name="kl_bank", tag="e")
+                word_transposes(
+                    bank, [rows_words[:, 2 * half + r, g * 2 * P : (g + 1) * 2 * P] for r in range(2)]
                 )
+                regrouped = grouped_words[:, half * 2 * P : (half + 1) * 2 * P, :].rearrange(
+                    "p (r c) u -> p r c u", r=2
+                )
+                if half == 0:
+                    nc.vector.tensor_copy(out=regrouped, in_=bank[:].rearrange("p r u c -> p r c u"))
+                else:
+                    nc.scalar.copy(out=regrouped, in_=bank[:].rearrange("p r u c -> p r c u"))
+            return grouped
 
         h_codes = keep.tile([P, D_PASSES, S], U32, name="h_codes", align_bytes=64)
         h_scales = keep.tile([P, D_PASSES, S], U8, name="h_scales", align_bytes=64)
@@ -195,27 +220,38 @@ def tile_attention_pb_kernel(
         v_codes = keep.tile([P, H * HD], U32, name="v_codes", align_bytes=64)
         v_scales = keep.tile([P, H * HD], U8, name="v_scales", align_bytes=64)
 
-        def project_values(half):
-            for a in range(QUAD):
-                h = half * QUAD + a
-                d_cols = slice(h * HD, (h + 1) * HD)
-                v_bank = psum_e.tile([P, ROW_TILES, HD], F32, name="v_bank", tag="e")
-                for t in range(ROW_TILES):
-                    j_cols = slice(t * P, (t + 1) * P)
-                    for g in range(D_PASSES):
-                        nc.tensor.matmul_mx(
-                            out=v_bank[:, t, :],
-                            lhsT=h_codes[:, g, j_cols].bitcast(FP8X4),
-                            lhsT_scale=h_scales[:, g, j_cols],
-                            rhs=w_codes[:, g, d_cols].bitcast(FP8X4),
-                            rhs_scale=w_scales[:, g, d_cols],
-                            start=(g == 0),
-                            stop=(g == D_PASSES - 1),
-                        )
-                if h % 2 == 0:
-                    nc.vector.tensor_copy(out=v_grouped[:, h, :, :], in_=v_bank[:].rearrange("p t d -> p d t"))
-                else:
-                    nc.scalar.copy(out=v_grouped[:, h, :, :], in_=v_bank[:].rearrange("p t d -> p d t"))
+        def quantise_512_rows(grouped, codes, scales):
+            nc.vector.quantize_mx(
+                out=codes.bitcast(FP8X4), scales=scales, in_=grouped[:].rearrange("p c t -> p (c t)")
+            )
+
+        v_banks = {}
+
+        def project(h):
+            d_cols = slice(h * HD, (h + 1) * HD)
+            v_bank = psum_e.tile([P, ROW_TILES, HD], F32, name="v_bank", tag="e")
+            for t in range(ROW_TILES):
+                j_cols = slice(t * P, (t + 1) * P)
+                for g in range(D_PASSES):
+                    nc.tensor.matmul_mx(
+                        out=v_bank[:, t, :],
+                        lhsT=h_codes[:, g, j_cols].bitcast(FP8X4),
+                        lhsT_scale=h_scales[:, g, j_cols],
+                        rhs=w_codes[:, g, d_cols].bitcast(FP8X4),
+                        rhs_scale=w_scales[:, g, d_cols],
+                        start=(g == 0),
+                        stop=(g == D_PASSES - 1),
+                    )
+            v_banks[h] = v_bank
+
+        def regroup_v(h):
+            v_bank = v_banks.pop(h)
+            if h % 2 == 0:
+                nc.vector.tensor_copy(out=v_grouped[:, h, :, :], in_=v_bank[:].rearrange("p t d -> p d t"))
+            else:
+                nc.scalar.copy(out=v_grouped[:, h, :, :], in_=v_bank[:].rearrange("p t d -> p d t"))
+
+        def quantise_v(half):
             cols = slice(half * QUAD * HD, (half + 1) * QUAD * HD)
             nc.vector.quantize_mx(
                 out=v_codes[:, cols].bitcast(FP8X4),
@@ -223,137 +259,229 @@ def tile_attention_pb_kernel(
                 in_=v_grouped[:, half * QUAD : (half + 1) * QUAD, :, :].rearrange("p a d t -> p (a d t)"),
             )
 
-        def scores(it, h):
+        unit_tiles = {}
+
+        def energies(k):
+            it, h = divmod(k, H)
             n = (it + 1) * P
             rows = slice(it * P, n)
-            shift = small.tile([P, C], F32, name="shift")
-            sums = small.tile([P, C], F32, name="sums")
-            recip = small.tile([P, C], F32, name="recip")
-            energy = []
+            if C * n <= S:
+                both = psum_e.tile([P, C, n], F32, name="e", tag="e")
+                energy = [both[:, c, :] for c in range(C)]
+            else:
+                energy = [psum_e.tile([P, n], F32, name="e", tag="e")[:] for c in range(C)]
             for c in range(C):
                 hc = h * C + c
-                e = psum_e.tile([P, S], F32, name="e", tag="e")
-                nc.tensor.matmul(e[:, :n], lhsT=qT[:, hc, rows], rhs=kT[:, hc, :n], start=True, stop=False)
-                nc.tensor.matmul(e[:, rows], lhsT=ident_bf[:], rhs=mask_bf[:], start=False, stop=True)
+                nc.tensor.matmul(energy[c], lhsT=qT[:, hc, rows], rhs=kT[:, hc, :n], start=True, stop=False)
+                nc.tensor.matmul(energy[c][:, rows], lhsT=ident_bf[:], rhs=mask_bf[:], start=False, stop=True)
+            unit_tiles[k] = {"energy": energy}
+
+        def maxima(k):
+            n = (k // H + 1) * P
+            shift = small.tile([P, C], F32, name="shift")
+            for c in range(C):
                 neg_scaled = work.tile([P, S], BF16, name="neg_scaled", bufs=3)
                 nc.vector.tensor_scalar(
                     out=neg_scaled[:, :n],
-                    in0=e[:, :n],
+                    in0=unit_tiles[k]["energy"][c],
                     scalar1=-SM_SCALE,
                     scalar2=None,
                     op0=ALU.mult,
                     op1=ALU.min,
                     accum_out=shift[:, c : c + 1],
                 )
-                energy.append(e)
+            unit_tiles[k]["shift"] = shift
+
+        def exponentials(k):
+            n = (k // H + 1) * P
+            sums = small.tile([P, C], F32, name="sums")
             probs = []
             for c in range(C):
                 p = work.tile([P, S], F32, name="p%d" % c, bufs=4)
                 nc.scalar.activation(
                     out=p[:, :n],
-                    in_=energy[c][:, :n],
+                    in_=unit_tiles[k]["energy"][c],
                     func=ACT.Exp,
-                    bias=shift[:, c : c + 1],
+                    bias=unit_tiles[k]["shift"][:, c : c + 1],
                     scale=SM_SCALE,
                     accum_out=sums[:, c : c + 1],
                 )
                 probs.append(p)
-            nc.vector.reciprocal(out=recip[:], in_=sums[:])
-            nc.vector.tensor_scalar(
-                out=probs[1][:, :n],
-                in0=probs[1][:, :n],
+            unit_tiles[k]["sums"] = sums
+            unit_tiles[k]["probs"] = probs
+
+        def rescale(k):
+            it, h = divmod(k, H)
+            n = (it + 1) * P
+            recip = small.tile([P, C], F32, name="recip")
+            nc.vector.reciprocal(out=recip[:], in_=unit_tiles[k]["sums"][:])
+            p1 = unit_tiles[k]["probs"][1]
+            nc.gpsimd.tensor_scalar(
+                out=p1[:, :n],
+                in0=p1[:, :n],
                 scalar1=recip[:, 1:2],
                 scalar2=scale_all[:, h : h + 1],
                 op0=ALU.mult,
                 op1=ALU.mult,
             )
+            unit_tiles[k]["recip"] = recip
+
+        def join(k):
+            it, h = divmod(k, H)
+            n = (it + 1) * P
+            tiles = unit_tiles.pop(k)
             nc.vector.scalar_tensor_tensor(
                 out=sc_sb[h][:, :n],
-                in0=probs[0][:, :n],
-                scalar=recip[:, 0:1],
-                in1=probs[1][:, :n],
+                in0=tiles["probs"][0][:, :n],
+                scalar=tiles["recip"][:, 0:1],
+                in1=tiles["probs"][1][:, :n],
                 op0=ALU.mult,
                 op1=ALU.add,
             )
 
-        def quantise_scores(pair):
+        pair_tiles = {}
+        out_rows = out.rearrange("b s h d -> (b s) (h d)")
+
+        def flip_scores(m):
+            first = (m * PAIR) % H
             bank = psum_t.tile([P, PAIR, 2, P], F32, name="sc_bank", tag="t")
-            word_transposes(bank, [sc_sb[pair * PAIR + r][:].bitcast(F32) for r in range(PAIR)])
+            word_transposes(bank, [sc_sb[first + r][:].bitcast(F32) for r in range(PAIR)])
+            pair_tiles[m] = {"bank": bank}
+
+        def regroup_scores(m):
             sc_grouped = work.tile([P, PAIR, P, PACK], BF16, name="sc_grouped", align_bytes=64)
-            nc.scalar.copy(out=sc_grouped[:].bitcast(F32), in_=bank[:].rearrange("p r u c -> p r c u"))
-            sc_codes = work.tile([P, PAIR * P], U32, name="sc_codes", bufs=6, align_bytes=64)
-            sc_scales = work.tile([P, PAIR * P], U8, name="sc_scales", bufs=6, align_bytes=64)
+            nc.scalar.copy(
+                out=sc_grouped[:].bitcast(F32), in_=pair_tiles[m]["bank"][:].rearrange("p r u c -> p r c u")
+            )
+            pair_tiles[m]["grouped"] = sc_grouped
+
+        def quantise_scores(m):
+            sc_codes = work.tile([P, PAIR * P], U32, name="sc_codes", bufs=3, align_bytes=64)
+            sc_scales = work.tile([P, PAIR * P], U8, name="sc_scales", bufs=3, align_bytes=64)
             nc.vector.quantize_mx(
                 out=sc_codes[:].bitcast(FP8X4),
                 scales=sc_scales[:],
-                in_=sc_grouped[:].rearrange("p r c t -> p (r c t)"),
+                in_=pair_tiles[m]["grouped"][:].rearrange("p r c t -> p (r c t)"),
             )
-            return sc_codes, sc_scales
+            pair_tiles[m]["codes"] = sc_codes
+            pair_tiles[m]["scales"] = sc_scales
 
-        out_rows = out.rearrange("b s h d -> (b s) (h d)")
-
-        def attend(it, pair, sc_codes, sc_scales):
+        def multiply(m):
+            first = (m * PAIR) % H
             att = psum_att.tile([P, PAIR, HD], F32, name="att", tag="att")
             for r in range(PAIR):
-                h = pair * PAIR + r
                 i_cols = slice(r * P, (r + 1) * P)
-                d_cols = slice(h * HD, (h + 1) * HD)
+                d_cols = slice((first + r) * HD, (first + r + 1) * HD)
                 nc.tensor.matmul_mx(
                     out=att[:, r, :],
-                    lhsT=sc_codes[:, i_cols].bitcast(FP8X4),
-                    lhsT_scale=sc_scales[:, i_cols],
+                    lhsT=pair_tiles[m]["codes"][:, i_cols].bitcast(FP8X4),
+                    lhsT_scale=pair_tiles[m]["scales"][:, i_cols],
                     rhs=v_codes[:, d_cols].bitcast(FP8X4),
                     rhs_scale=v_scales[:, d_cols],
                     start=True,
                     stop=True,
                 )
+            pair_tiles[m]["att"] = att
+
+        def square_sums(m):
             squares = work.tile([P, PAIR, HD], BF16, name="squares")
             sum_sq = small.tile([P, PAIR], F32, name="sum_sq")
             for r in range(PAIR):
                 nc.scalar.activation(
-                    out=squares[:, r, :], in_=att[:, r, :], func=ACT.Square, accum_out=sum_sq[:, r : r + 1]
+                    out=squares[:, r, :],
+                    in_=pair_tiles[m]["att"][:, r, :],
+                    func=ACT.Square,
+                    accum_out=sum_sq[:, r : r + 1],
                 )
+            pair_tiles[m]["sum_sq"] = sum_sq
+
+        def inverse_rms(m):
             mean_sq = small.tile([P, PAIR], F32, name="mean_sq")
             nc.gpsimd.tensor_scalar(
-                out=mean_sq[:], in0=sum_sq[:], scalar1=1.0 / HD, scalar2=EPS, op0=ALU.mult, op1=ALU.add
+                out=mean_sq[:],
+                in0=pair_tiles[m]["sum_sq"][:],
+                scalar1=1.0 / HD,
+                scalar2=EPS,
+                op0=ALU.mult,
+                op1=ALU.add,
             )
             rstd = small.tile([P, PAIR], F32, name="rstd")
             nc.gpsimd.tensor_tensor(out=rstd[:], in0=mean_sq[:], in1=neg_half[:], op=ALU.pow)
+            pair_tiles[m]["rstd"] = rstd
+
+        def finish(m):
+            it, first = divmod(m * PAIR, H)
+            tiles = pair_tiles.pop(m)
             normed = work.tile([P, PAIR, HD], F32, name="normed", bufs=3)
             for r in range(PAIR):
                 nc.vector.scalar_tensor_tensor(
                     out=normed[:, r, :],
-                    in0=att[:, r, :],
-                    scalar=rstd[:, r : r + 1],
-                    in1=gain[:, pair * PAIR + r, :],
+                    in0=tiles["att"][:, r, :],
+                    scalar=tiles["rstd"][:, r : r + 1],
+                    in1=gain[:, first + r, :],
                     op0=ALU.mult,
                     op1=ALU.mult,
                 )
             nc.sync.dma_start(
-                out=out_rows[it * P : (it + 1) * P, pair * PAIR * HD : (pair + 1) * PAIR * HD],
+                out=out_rows[it * P : (it + 1) * P, first * HD : (first + PAIR) * HD],
                 in_=normed[:].rearrange("p r d -> p (r d)"),
             )
 
-        def scores_of_two_heads(it, pair):
-            for r in range(PAIR):
-                scores(it, pair * PAIR + r)
-            if it + 1 < ROW_TILES:
-                transpose_qk(it + 1, pair)
-            return quantise_scores(pair)
+        def unit_at(slot, lag, stage):
+            k = slot - lag
+            if 0 <= k < UNITS:
+                stage(k)
 
-        for piece in range(4):
-            transpose_qk(0, piece)
-        tile0 = [scores_of_two_heads(0, pair) for pair in range(H // PAIR)]
-        quantise_512_rows(h_sb[:].bitcast(F32), h_codes, h_scales)
+        def head_at(slot, lag, stage):
+            h = slot - lag
+            if 0 <= h < H:
+                stage(h)
+
+        def piece_at(slot, lag, stage):
+            it, rest = divmod(slot - lag, H)
+            if 0 <= it < ROW_TILES - 1 and rest % 2 == 1:
+                stage(it + 1, rest // 2)
+
+        def pair_at(slot, lag, stage):
+            m, odd = divmod(slot - lag, PAIR)
+            if odd == 0 and 0 <= m < PAIRS:
+                stage(m)
+
+        to_quantise = []
+        blocks = [(h_sb[:].bitcast(F32), h_codes, h_scales)]
         for half in range(H // QUAD):
             heads = slice(half * QUAD, (half + 1) * QUAD)
             cols = slice(half * QUAD * HD, (half + 1) * QUAD * HD)
-            quantise_512_rows(w_sb[:, heads, :].bitcast(F32), w_codes[:, :, cols], w_scales[:, :, cols])
-        for half in range(H // QUAD):
-            project_values(half)
-        for pair in range(H // PAIR):
-            attend(0, pair, tile0[pair][0], tile0[pair][1])
-        for it in range(1, ROW_TILES):
-            for pair in range(H // PAIR):
-                sc_codes, sc_scales = scores_of_two_heads(it, pair)
-                attend(it, pair, sc_codes, sc_scales)
+            blocks.append((w_sb[:, heads, :].bitcast(F32), w_codes[:, :, cols], w_scales[:, :, cols]))
+        for b, (rows_words, codes, scales) in enumerate(blocks):
+            for g in range(D_PASSES):
+                to_quantise.append((regroup_512_rows(rows_words, g), codes[:, g, :], scales[:, g, :]))
+                if len(to_quantise) > 1:
+                    quantise_512_rows(*to_quantise.pop(0))
+            if b == 0:
+                head_factors()
+            if b == 1:
+                for piece in range(4):
+                    flip_qk(0, piece)
+                    keep_qk(0, piece, on_vector=(piece % 2 == 0))
+        quantise_512_rows(*to_quantise.pop(0))
+
+        for slot in range(LAG_ENERGY, UNITS + LAG_FINISH):
+            unit_at(slot, LAG_ENERGY, energies)
+            head_at(slot, 0, project)
+            pair_at(slot, LAG_MULTIPLY, multiply)
+            pair_at(slot, LAG_FLIP, flip_scores)
+            piece_at(slot, 0, flip_qk)
+            unit_at(slot, LAG_EXP, exponentials)
+            unit_at(slot, LAG_RESCALE, rescale)
+            unit_at(slot, LAG_JOIN, join)
+            head_at(slot, 1, regroup_v)
+            piece_at(slot, 1, keep_qk)
+            pair_at(slot, LAG_REGROUP, regroup_scores)
+            pair_at(slot, LAG_SQUARES, square_sums)
+            if slot in (QUAD + 1, 2 * QUAD + 1):
+                quantise_v(slot // QUAD - 1)
+            pair_at(slot, LAG_QUANTISE, quantise_scores)
+            pair_at(slot, LAG_RMS, inverse_rms)
+            pair_at(slot, LAG_FINISH, finish)
+            unit_at(slot, LAG_ENERGY, maxima)

@@ -33,6 +33,7 @@ LAG_ENERGY = -1
 LAG_EXP = 0
 LAG_RESCALE = 1
 LAG_JOIN = 2
+LAG_PROJECT = 1
 LAG_FLIP = 4
 LAG_REGROUP = 5
 LAG_QUANTISE = 6
@@ -61,18 +62,17 @@ def tile_attention_pb_kernel(
 
         qk_vec = consts.tile([H, 4, HD], BF16, name="qk_vec")
         for n, vec in enumerate((q1, q2, k1, k2)):
-            nc.sync.dma_start(out=qk_vec[:, n, :], in_=vec.rearrange("h d o -> h (d o)"))
+            nc.scalar.dma_start(out=qk_vec[:, n, :], in_=vec.rearrange("h d o -> h (d o)"))
+        row0 = consts.tile([P, 2 * P], BF16, name="row0")
+        nc.vector.memset(row0[:], 0.0)
+        nc.scalar.dma_start(out=row0[0:1, 0:HD], in_=head_norm_w.rearrange("(o d) -> o d", o=1))
+        nc.scalar.dma_start(out=row0[0:1, P : P + H], in_=lam_init.rearrange("(o h) -> o h", o=1))
 
         h_sb = loads.tile([P, ROW_TILES, D], BF16, name="h_sb")
         h_halves = h_sb[:].rearrange("p (u e) k -> p u (e k)", u=2)
         h_rows = h_norm.rearrange("b s k -> (b s) k").rearrange("(u p e) k -> p u (e k)", u=2, e=2)
         for u in range(2):
             nc.sync.dma_start(out=h_halves[:, u, :], in_=h_rows[:, u, :])
-
-        lam_all = consts.tile([P, H], BF16, name="lam_all")
-        nc.sync.dma_start(out=lam_all[:], in_=lam_init.partition_broadcast(P))
-        w_all = consts.tile([P, HD], BF16, name="w_all")
-        nc.sync.dma_start(out=w_all[:], in_=head_norm_w.partition_broadcast(P))
 
         w_sb = loads.tile([P, H, D], BF16, name="w_sb")
         w_tiles = wv.rearrange("(o p) k -> p o k", p=P)
@@ -115,6 +115,8 @@ def tile_attention_pb_kernel(
             pattern=[[-1, P]],
             channel_multiplier=1,
         )
+        ones_bf = consts.tile([P, P], BF16, name="ones_bf")
+        nc.vector.memset(ones_bf[:], 1.0)
         neg_half = consts.tile([P, PAIR], F32, name="neg_half")
         nc.vector.memset(neg_half[:], -0.5)
         warm = consts.tile([P, 1], F32, name="warm")
@@ -142,8 +144,14 @@ def tile_attention_pb_kernel(
             nc.tensor.matmul(
                 base_all[:], lhsT=base[:, 0:1].to_broadcast([P, P]), rhs=ident_f32[:], start=True, stop=True
             )
+            row_bank = psum_att.tile([P, 2 * P], F32, name="row_bank", tag="att")
+            nc.tensor.matmul(row_bank[:], lhsT=ones_bf[:], rhs=row0[:], start=True, stop=True)
+            row_all = consts.tile([P, P + H], F32, name="row_all")
+            nc.vector.tensor_copy(out=row_all[:], in_=row_bank[:, 0 : P + H])
+            w_all = row_all[:, 0:HD]
+            lam_all = row_all[:, P : P + H]
             lam_sum = consts.tile([P, 1], F32, name="lam_sum")
-            nc.vector.reduce_sum(out=lam_sum[:], in_=lam_all[:], axis=AX.X)
+            nc.vector.reduce_sum(out=lam_sum[:], in_=lam_all, axis=AX.X)
             nc.vector.tensor_scalar(
                 out=scale_all[:],
                 in0=base_all[:, 0:H],
@@ -154,12 +162,12 @@ def tile_attention_pb_kernel(
             )
             one_minus_lam = consts.tile([P, H], F32, name="one_minus_lam")
             nc.gpsimd.tensor_scalar(
-                out=one_minus_lam[:], in0=lam_all[:], scalar1=-1.0, scalar2=1.0, op0=ALU.mult, op1=ALU.add
+                out=one_minus_lam[:], in0=lam_all, scalar1=-1.0, scalar2=1.0, op0=ALU.mult, op1=ALU.add
             )
             for h in range(H):
                 nc.gpsimd.tensor_scalar(
                     out=gain[:, h, :],
-                    in0=w_all[:],
+                    in0=w_all,
                     scalar1=one_minus_lam[:, h : h + 1],
                     scalar2=0.0,
                     op0=ALU.mult,
@@ -195,21 +203,21 @@ def tile_attention_pb_kernel(
                 for u in range(2):
                     nc.tensor.transpose(bank[:, r, u, :], pair_words[r][:, u * P : (u + 1) * P], ident_f32[:])
 
-        def regroup_512_rows(rows_words, g):
-            grouped = work.tile([P, QUAD * P, PACK], BF16, name="grouped", bufs=3, align_bytes=64)
-            grouped_words = grouped[:].bitcast(F32)
+        def flip_512_rows(rows_words, g, pool, tag):
+            banks = []
             for half in range(2):
-                bank = psum_e.tile([P, 2, 2, P], F32, name="kl_bank", tag="e")
+                bank = pool.tile([P, 2, 2, P], F32, name="kl_bank", tag=tag)
                 word_transposes(
                     bank, [rows_words[:, 2 * half + r, g * 2 * P : (g + 1) * 2 * P] for r in range(2)]
                 )
-                regrouped = grouped_words[:, half * 2 * P : (half + 1) * 2 * P, :].rearrange(
-                    "p (r c) u -> p r c u", r=2
-                )
-                if half == 0:
-                    nc.vector.tensor_copy(out=regrouped, in_=bank[:].rearrange("p r u c -> p r c u"))
-                else:
-                    nc.scalar.copy(out=regrouped, in_=bank[:].rearrange("p r u c -> p r c u"))
+                banks.append(bank)
+            return banks
+
+        def regroup_512_rows(banks):
+            grouped = work.tile([P, QUAD * P, PACK], BF16, name="grouped", bufs=3, align_bytes=64)
+            halves = grouped[:].bitcast(F32).rearrange("p (a r c) u -> p a r c u", a=2, r=2)
+            nc.vector.tensor_copy(out=halves[:, 0], in_=banks[0][:].rearrange("p r u c -> p r c u"))
+            nc.scalar.copy(out=halves[:, 1], in_=banks[1][:].rearrange("p r u c -> p r c u"))
             return grouped
 
         h_codes = keep.tile([P, D_PASSES, S], U32, name="h_codes", align_bytes=64)
@@ -447,40 +455,61 @@ def tile_attention_pb_kernel(
             if odd == 0 and 0 <= m < PAIRS:
                 stage(m)
 
-        to_quantise = []
-        blocks = [(h_sb[:].bitcast(F32), h_codes, h_scales)]
-        for half in range(H // QUAD):
+        def w_half(half):
             heads = slice(half * QUAD, (half + 1) * QUAD)
             cols = slice(half * QUAD * HD, (half + 1) * QUAD * HD)
-            blocks.append((w_sb[:, heads, :].bitcast(F32), w_codes[:, :, cols], w_scales[:, :, cols]))
-        for b, (rows_words, codes, scales) in enumerate(blocks):
+            return w_sb[:, heads, :].bitcast(F32), w_codes[:, :, cols], w_scales[:, :, cols]
+
+        to_quantise = []
+        for rows_words, codes, scales in ((h_sb[:].bitcast(F32), h_codes, h_scales), w_half(0)):
             for g in range(D_PASSES):
-                to_quantise.append((regroup_512_rows(rows_words, g), codes[:, g, :], scales[:, g, :]))
+                grouped = regroup_512_rows(flip_512_rows(rows_words, g, psum_e, "e"))
+                to_quantise.append((grouped, codes[:, g, :], scales[:, g, :]))
                 if len(to_quantise) > 1:
                     quantise_512_rows(*to_quantise.pop(0))
-            if b == 0:
-                head_factors()
-            if b == 1:
-                for piece in range(4):
-                    flip_qk(0, piece)
-                    keep_qk(0, piece, on_vector=(piece % 2 == 0))
-        quantise_512_rows(*to_quantise.pop(0))
+        head_factors()
+        for piece in range(4):
+            flip_qk(0, piece)
+            if piece == 0:
+                quantise_512_rows(*to_quantise.pop(0))
+            keep_qk(0, piece, on_vector=(piece % 2 == 0))
+
+        late_words, late_codes, late_scales = w_half(1)
+        late = {}
+
+        def flip_late(g):
+            late[g] = flip_512_rows(late_words, g, psum_att, "att")
+
+        def regroup_late(g):
+            late[g] = regroup_512_rows(late[g])
+
+        def quantise_late(g):
+            quantise_512_rows(late.pop(g), late_codes[:, g, :], late_scales[:, g, :])
+
+        def pass_at(slot, lag, stage):
+            g = slot - lag
+            if 0 <= g < D_PASSES:
+                stage(g)
 
         for slot in range(LAG_ENERGY, UNITS + LAG_FINISH):
             unit_at(slot, LAG_ENERGY, energies)
-            head_at(slot, 0, project)
+            head_at(slot, LAG_PROJECT, project)
             pair_at(slot, LAG_MULTIPLY, multiply)
+            pass_at(slot, 1, flip_late)
             pair_at(slot, LAG_FLIP, flip_scores)
             piece_at(slot, 0, flip_qk)
             unit_at(slot, LAG_EXP, exponentials)
             unit_at(slot, LAG_RESCALE, rescale)
             unit_at(slot, LAG_JOIN, join)
-            head_at(slot, 1, regroup_v)
+            pass_at(slot, 2, regroup_late)
+            head_at(slot, LAG_PROJECT + 1, regroup_v)
             piece_at(slot, 1, keep_qk)
             pair_at(slot, LAG_REGROUP, regroup_scores)
             pair_at(slot, LAG_SQUARES, square_sums)
-            if slot in (QUAD + 1, 2 * QUAD + 1):
-                quantise_v(slot // QUAD - 1)
+            pass_at(slot, 3, quantise_late)
+            for half in range(H // QUAD):
+                if slot == LAG_PROJECT + 1 + (half + 1) * QUAD:
+                    quantise_v(half)
             pair_at(slot, LAG_QUANTISE, quantise_scores)
             pair_at(slot, LAG_RMS, inverse_rms)
             pair_at(slot, LAG_FINISH, finish)

@@ -25,6 +25,7 @@ QUAD = 4
 PAIR = 2
 UNITS = ROW_TILES * H
 PAIRS = UNITS // PAIR
+QUADS = UNITS // QUAD
 SM_SCALE = 1.0 / (HD ** 0.5)
 EPS = 1e-9
 MASKED = -1.0e30
@@ -33,14 +34,18 @@ LAG_ENERGY = -1
 LAG_EXP = 0
 LAG_RESCALE = 1
 LAG_JOIN = 2
-LAG_PROJECT = 1
 LAG_FLIP = 4
 LAG_REGROUP = 5
 LAG_QUANTISE = 6
 LAG_MULTIPLY = 7
-LAG_SQUARES = 8
-LAG_RMS = 9
-LAG_FINISH = 10
+LAG_SQUARES = 1
+LAG_RMS = 2
+LAG_FINISH = 3
+VALUE_PASSES = 6
+SLOT_FACTORS = -1
+SLOT_VALUE_PATH = 0
+SLOT_PROJECT = 7
+SLOT_VALUES = 11
 
 FLOPS = 2 * S * D * H * HD + 2 * H * C * S * S * HD + 2 * H * S * S * HD
 
@@ -60,50 +65,52 @@ def tile_attention_pb_kernel(
         psum_att = ctx.enter_context(tc.psum_pool(name="psum_att", bufs=2))
         ctx.enter_context(tc.manual_schedule())
 
-        qk_vec = consts.tile([H, 4, HD], BF16, name="qk_vec")
-        for n, vec in enumerate((q1, q2, k1, k2)):
-            nc.scalar.dma_start(out=qk_vec[:, n, :], in_=vec.rearrange("h d o -> h (d o)"))
+        neg_half = consts.tile([P, QUAD], F32, name="neg_half")
+        nc.vector.memset(neg_half[:], -0.5)
+        ident_bf = consts.tile([P, P], BF16, name="ident_bf")
+        nc.vector.memset(ident_bf[:], 0.0)
+        make_identity(nc, ident_bf[:], nomemset=True)
         row0 = consts.tile([P, 2 * P], BF16, name="row0")
         nc.vector.memset(row0[:], 0.0)
-        nc.scalar.dma_start(out=row0[0:1, 0:HD], in_=head_norm_w.rearrange("(o d) -> o d", o=1))
-        nc.scalar.dma_start(out=row0[0:1, P : P + H], in_=lam_init.rearrange("(o h) -> o h", o=1))
-
-        h_sb = loads.tile([P, ROW_TILES, D], BF16, name="h_sb")
-        h_halves = h_sb[:].rearrange("p (u e) k -> p u (e k)", u=2)
-        h_rows = h_norm.rearrange("b s k -> (b s) k").rearrange("(u p e) k -> p u (e k)", u=2, e=2)
-        for u in range(2):
-            nc.sync.dma_start(out=h_halves[:, u, :], in_=h_rows[:, u, :])
-
-        w_sb = loads.tile([P, H, D], BF16, name="w_sb")
-        w_tiles = wv.rearrange("(o p) k -> p o k", p=P)
-
-        def load_w(half):
-            for first in range(half * QUAD, (half + 1) * QUAD, PAIR):
-                heads = slice(first, first + PAIR)
-                nc.sync.dma_start(out=w_sb[:, heads, :], in_=w_tiles[:, heads, :])
 
         q_rows = q_rot.rearrange("b s h m -> (b s) (h m)")
         k_rows = k_rot.rearrange("b s h m -> (b s) (h m)")
         q_sb = [loads.tile([P, H * C * HD], BF16, name="q_sb%d" % it) for it in range(ROW_TILES)]
         k_sb = [loads.tile([P, H * C * HD], BF16, name="k_sb%d" % it) for it in range(ROW_TILES)]
 
-        def load_qk(it):
+        def load_qk(it, cols):
             rows = slice(it * P, (it + 1) * P)
-            nc.sync.dma_start(out=q_sb[it][:], in_=q_rows[rows, :])
-            nc.sync.dma_start(out=k_sb[it][:], in_=k_rows[rows, :])
+            nc.sync.dma_start(out=q_sb[it][:, cols], in_=q_rows[rows, cols])
+            nc.sync.dma_start(out=k_sb[it][:, cols], in_=k_rows[rows, cols])
 
-        load_w(0)
-        load_qk(0)
-        load_w(1)
+        half_cols = H * C * HD // 2
+        load_qk(0, slice(0, half_cols))
+
+        qk_vec = consts.tile([H, 4, HD], BF16, name="qk_vec")
+        for n, vec in enumerate((q1, q2, k1, k2)):
+            nc.scalar.dma_start(out=qk_vec[:, n, :], in_=vec.rearrange("h d o -> h (d o)"))
+        nc.scalar.dma_start(out=row0[0:1, 0:HD], in_=head_norm_w.rearrange("(o d) -> o d", o=1))
+        nc.scalar.dma_start(out=row0[0:1, P : P + H], in_=lam_init.rearrange("(o h) -> o h", o=1))
+
+        warm = consts.tile([P, 1], F32, name="warm")
+        nc.scalar.activation(out=warm[:], in_=neg_half[:, 0:1], func=ACT.Exp)
+
+        load_qk(0, slice(half_cols, 2 * half_cols))
+        h_sb = loads.tile([P, ROW_TILES, D], BF16, name="h_sb")
+        h_halves = h_sb[:].rearrange("p (u e) k -> p u (e k)", u=2)
+        h_rows = h_norm.rearrange("b s k -> (b s) k").rearrange("(u p e) k -> p u (e k)", u=2, e=2)
+        for u in range(2):
+            nc.sync.dma_start(out=h_halves[:, u, :], in_=h_rows[:, u, :])
+        w_sb = loads.tile([P, H, D], BF16, name="w_sb")
+        w_tiles = wv.rearrange("(o p) k -> p o k", p=P)
+        for first in range(0, H, PAIR):
+            heads = slice(first, first + PAIR)
+            nc.sync.dma_start(out=w_sb[:, heads, :], in_=w_tiles[:, heads, :])
         for it in range(1, ROW_TILES):
-            load_qk(it)
+            load_qk(it, slice(0, 2 * half_cols))
 
-        ident_f32 = consts.tile([P, P], F32, name="ident_f32")
-        nc.vector.memset(ident_f32[:], 0.0)
-        make_identity(nc, ident_f32[:], nomemset=True)
-        ident_bf = consts.tile([P, P], BF16, name="ident_bf")
-        nc.vector.memset(ident_bf[:], 0.0)
-        make_identity(nc, ident_bf[:], nomemset=True)
+        sc_sb = keep.tile([P, H, S], BF16, name="sc_sb")
+        nc.vector.memset(sc_sb[:].rearrange("p h s -> p (h s)").bitcast(U32), 0)
         mask_f32 = consts.tile([P, P], F32, name="mask_f32")
         nc.vector.memset(mask_f32[:], 0.0)
         nc.gpsimd.affine_select(
@@ -115,52 +122,62 @@ def tile_attention_pb_kernel(
             pattern=[[-1, P]],
             channel_multiplier=1,
         )
-        ones_bf = consts.tile([P, P], BF16, name="ones_bf")
-        nc.vector.memset(ones_bf[:], 1.0)
-        neg_half = consts.tile([P, PAIR], F32, name="neg_half")
-        nc.vector.memset(neg_half[:], -0.5)
-        warm = consts.tile([P, 1], F32, name="warm")
-        nc.scalar.activation(out=warm[:], in_=neg_half[:, 0:1], func=ACT.Exp)
-        sc_sb = [keep.tile([P, S], BF16, name="sc_sb%d" % h) for h in range(H)]
-        for h in range(H):
-            nc.vector.memset(sc_sb[h][:], 0.0)
-        base = consts.tile([P, 1], F32, name="base")
-        nc.vector.memset(base[:], 0.0)
         mask_bf = consts.tile([P, P], BF16, name="mask_bf")
         nc.vector.tensor_copy(out=mask_bf[:], in_=mask_f32[:])
+        ident_f32 = consts.tile([P, P], F32, name="ident_f32")
+        nc.vector.memset(ident_f32[:], 0.0)
+        make_identity(nc, ident_f32[:], nomemset=True)
+        ones_bf = consts.tile([P, P], BF16, name="ones_bf")
+        nc.vector.memset(ones_bf[:], 1.0)
+        base = consts.tile([P, 1], F32, name="base")
+        nc.vector.memset(base[:], 0.0)
 
         scale_all = consts.tile([P, H], F32, name="scale_all")
         gain = consts.tile([P, H, HD], F32, name="gain")
 
-        def head_factors():
+        dots = consts.tile([H, 2], F32, name="dots")
+        exps = consts.tile([H, 2], F32, name="exps")
+        one_minus_lam = consts.tile([P, H], F32, name="one_minus_lam")
+        row_all = consts.tile([P, P + H], F32, name="row_all")
+        w_all = row_all[:, 0:HD]
+        lam_all = row_all[:, P : P + H]
+        factor_banks = {}
+
+        def factor_dots():
             prod = consts.tile([H, 2, HD], F32, name="prod")
             nc.vector.tensor_tensor(out=prod[:], in0=qk_vec[:, 0:2, :], in1=qk_vec[:, 2:4, :], op=ALU.mult)
-            dots = consts.tile([H, 2], F32, name="dots")
             nc.vector.reduce_sum(out=dots[:], in_=prod[:], axis=AX.X)
-            exps = consts.tile([H, 2], F32, name="exps")
+
+        def factor_exps():
             nc.scalar.activation(out=exps[:], in_=dots[:], func=ACT.Exp)
+
+        def factor_bases():
             nc.vector.tensor_sub(out=base[0:H, :], in0=exps[:, 0:1], in1=exps[:, 1:2])
+
+        def factor_spread():
             base_all = psum_att.tile([P, P], F32, name="base_all", tag="att")
             nc.tensor.matmul(
                 base_all[:], lhsT=base[:, 0:1].to_broadcast([P, P]), rhs=ident_f32[:], start=True, stop=True
             )
             row_bank = psum_att.tile([P, 2 * P], F32, name="row_bank", tag="att")
             nc.tensor.matmul(row_bank[:], lhsT=ones_bf[:], rhs=row0[:], start=True, stop=True)
-            row_all = consts.tile([P, P + H], F32, name="row_all")
-            nc.vector.tensor_copy(out=row_all[:], in_=row_bank[:, 0 : P + H])
-            w_all = row_all[:, 0:HD]
-            lam_all = row_all[:, P : P + H]
+            factor_banks["base"] = base_all
+            factor_banks["row"] = row_bank
+
+        def factor_scales():
+            nc.vector.tensor_copy(out=row_all[:], in_=factor_banks["row"][:, 0 : P + H])
             lam_sum = consts.tile([P, 1], F32, name="lam_sum")
             nc.vector.reduce_sum(out=lam_sum[:], in_=lam_all, axis=AX.X)
             nc.vector.tensor_scalar(
                 out=scale_all[:],
-                in0=base_all[:, 0:H],
+                in0=factor_banks["base"][:, 0:H],
                 scalar1=-float(H),
                 scalar2=lam_sum[:, 0:1],
                 op0=ALU.mult,
                 op1=ALU.subtract,
             )
-            one_minus_lam = consts.tile([P, H], F32, name="one_minus_lam")
+
+        def factor_gains():
             nc.gpsimd.tensor_scalar(
                 out=one_minus_lam[:], in0=lam_all, scalar1=-1.0, scalar2=1.0, op0=ALU.mult, op1=ALU.add
             )
@@ -203,10 +220,10 @@ def tile_attention_pb_kernel(
                 for u in range(2):
                     nc.tensor.transpose(bank[:, r, u, :], pair_words[r][:, u * P : (u + 1) * P], ident_f32[:])
 
-        def flip_512_rows(rows_words, g, pool, tag):
+        def flip_512_rows(rows_words, g):
             banks = []
             for half in range(2):
-                bank = pool.tile([P, 2, 2, P], F32, name="kl_bank", tag=tag)
+                bank = psum_att.tile([P, 2, 2, P], F32, name="kl_bank", tag="att")
                 word_transposes(
                     bank, [rows_words[:, 2 * half + r, g * 2 * P : (g + 1) * 2 * P] for r in range(2)]
                 )
@@ -237,7 +254,7 @@ def tile_attention_pb_kernel(
 
         def project(h):
             d_cols = slice(h * HD, (h + 1) * HD)
-            v_bank = psum_e.tile([P, ROW_TILES, HD], F32, name="v_bank", tag="e")
+            v_bank = psum_att.tile([P, ROW_TILES, HD], F32, name="v_bank", tag="att")
             for t in range(ROW_TILES):
                 j_cols = slice(t * P, (t + 1) * P)
                 for g in range(D_PASSES):
@@ -339,7 +356,7 @@ def tile_attention_pb_kernel(
             n = (it + 1) * P
             tiles = unit_tiles.pop(k)
             nc.vector.scalar_tensor_tensor(
-                out=sc_sb[h][:, :n],
+                out=sc_sb[:, h, :n],
                 in0=tiles["probs"][0][:, :n],
                 scalar=tiles["recip"][:, 0:1],
                 in1=tiles["probs"][1][:, :n],
@@ -348,12 +365,13 @@ def tile_attention_pb_kernel(
             )
 
         pair_tiles = {}
+        quad_tiles = {}
         out_rows = out.rearrange("b s h d -> (b s) (h d)")
 
         def flip_scores(m):
             first = (m * PAIR) % H
             bank = psum_t.tile([P, PAIR, 2, P], F32, name="sc_bank", tag="t")
-            word_transposes(bank, [sc_sb[first + r][:].bitcast(F32) for r in range(PAIR)])
+            word_transposes(bank, [sc_sb[:, first + r, :].bitcast(F32) for r in range(PAIR)])
             pair_tiles[m] = {"bank": bank}
 
         def regroup_scores(m):
@@ -364,8 +382,8 @@ def tile_attention_pb_kernel(
             pair_tiles[m]["grouped"] = sc_grouped
 
         def quantise_scores(m):
-            sc_codes = work.tile([P, PAIR * P], U32, name="sc_codes", bufs=3, align_bytes=64)
-            sc_scales = work.tile([P, PAIR * P], U8, name="sc_scales", bufs=3, align_bytes=64)
+            sc_codes = work.tile([P, PAIR * P], U32, name="sc_codes", bufs=4, align_bytes=64)
+            sc_scales = work.tile([P, PAIR * P], U8, name="sc_scales", bufs=4, align_bytes=64)
             nc.vector.quantize_mx(
                 out=sc_codes[:].bitcast(FP8X4),
                 scales=sc_scales[:],
@@ -376,52 +394,54 @@ def tile_attention_pb_kernel(
 
         def multiply(m):
             first = (m * PAIR) % H
-            att = psum_att.tile([P, PAIR, HD], F32, name="att", tag="att")
+            quad, second = divmod(m, 2)
+            if not second:
+                quad_tiles[quad] = {"att": psum_att.tile([P, QUAD, HD], F32, name="att", tag="att")}
+            tiles = pair_tiles.pop(m)
             for r in range(PAIR):
                 i_cols = slice(r * P, (r + 1) * P)
                 d_cols = slice((first + r) * HD, (first + r + 1) * HD)
                 nc.tensor.matmul_mx(
-                    out=att[:, r, :],
-                    lhsT=pair_tiles[m]["codes"][:, i_cols].bitcast(FP8X4),
-                    lhsT_scale=pair_tiles[m]["scales"][:, i_cols],
+                    out=quad_tiles[quad]["att"][:, second * PAIR + r, :],
+                    lhsT=tiles["codes"][:, i_cols].bitcast(FP8X4),
+                    lhsT_scale=tiles["scales"][:, i_cols],
                     rhs=v_codes[:, d_cols].bitcast(FP8X4),
                     rhs_scale=v_scales[:, d_cols],
                     start=True,
                     stop=True,
                 )
-            pair_tiles[m]["att"] = att
 
-        def square_sums(m):
-            squares = work.tile([P, PAIR, HD], BF16, name="squares")
-            sum_sq = small.tile([P, PAIR], F32, name="sum_sq")
-            for r in range(PAIR):
+        def square_sums(quad):
+            squares = work.tile([P, QUAD, HD], BF16, name="squares")
+            sum_sq = small.tile([P, QUAD], F32, name="sum_sq")
+            for r in range(QUAD):
                 nc.scalar.activation(
                     out=squares[:, r, :],
-                    in_=pair_tiles[m]["att"][:, r, :],
+                    in_=quad_tiles[quad]["att"][:, r, :],
                     func=ACT.Square,
                     accum_out=sum_sq[:, r : r + 1],
                 )
-            pair_tiles[m]["sum_sq"] = sum_sq
+            quad_tiles[quad]["sum_sq"] = sum_sq
 
-        def inverse_rms(m):
-            mean_sq = small.tile([P, PAIR], F32, name="mean_sq")
+        def inverse_rms(quad):
+            mean_sq = small.tile([P, QUAD], F32, name="mean_sq")
             nc.gpsimd.tensor_scalar(
                 out=mean_sq[:],
-                in0=pair_tiles[m]["sum_sq"][:],
+                in0=quad_tiles[quad]["sum_sq"][:],
                 scalar1=1.0 / HD,
                 scalar2=EPS,
                 op0=ALU.mult,
                 op1=ALU.add,
             )
-            rstd = small.tile([P, PAIR], F32, name="rstd")
+            rstd = small.tile([P, QUAD], F32, name="rstd")
             nc.gpsimd.tensor_tensor(out=rstd[:], in0=mean_sq[:], in1=neg_half[:], op=ALU.pow)
-            pair_tiles[m]["rstd"] = rstd
+            quad_tiles[quad]["rstd"] = rstd
 
-        def finish(m):
-            it, first = divmod(m * PAIR, H)
-            tiles = pair_tiles.pop(m)
-            normed = work.tile([P, PAIR, HD], F32, name="normed", bufs=3)
-            for r in range(PAIR):
+        def finish(quad):
+            it, first = divmod(quad * QUAD, H)
+            tiles = quad_tiles.pop(quad)
+            normed = work.tile([P, QUAD, HD], F32, name="normed", bufs=3)
+            for r in range(QUAD):
                 nc.vector.scalar_tensor_tensor(
                     out=normed[:, r, :],
                     in0=tiles["att"][:, r, :],
@@ -431,7 +451,7 @@ def tile_attention_pb_kernel(
                     op1=ALU.mult,
                 )
             nc.sync.dma_start(
-                out=out_rows[it * P : (it + 1) * P, first * HD : (first + PAIR) * HD],
+                out=out_rows[it * P : (it + 1) * P, first * HD : (first + QUAD) * HD],
                 in_=normed[:].rearrange("p r d -> p (r d)"),
             )
 
@@ -440,77 +460,98 @@ def tile_attention_pb_kernel(
             if 0 <= k < UNITS:
                 stage(k)
 
-        def head_at(slot, lag, stage):
-            h = slot - lag
-            if 0 <= h < H:
-                stage(h)
-
-        def piece_at(slot, lag, stage):
-            it, rest = divmod(slot - lag, H)
-            if 0 <= it < ROW_TILES - 1 and rest % 2 == 1:
-                stage(it + 1, rest // 2)
-
         def pair_at(slot, lag, stage):
             m, odd = divmod(slot - lag, PAIR)
             if odd == 0 and 0 <= m < PAIRS:
                 stage(m)
 
-        def w_half(half):
-            heads = slice(half * QUAD, (half + 1) * QUAD)
-            cols = slice(half * QUAD * HD, (half + 1) * QUAD * HD)
-            return w_sb[:, heads, :].bitcast(F32), w_codes[:, :, cols], w_scales[:, :, cols]
+        def multiply_slot(m):
+            return max(2 * m + LAG_MULTIPLY, SLOT_VALUES + m)
 
-        to_quantise = []
-        for rows_words, codes, scales in ((h_sb[:].bitcast(F32), h_codes, h_scales), w_half(0)):
+        def quad_at(slot, lag, stage):
+            for quad in range(QUADS):
+                if multiply_slot(2 * quad + 1) + lag == slot:
+                    stage(quad)
+
+        def piece_at(slot, lag, stage):
+            it, rest = divmod(slot - lag, H)
+            if 0 <= it < ROW_TILES - 1 and rest % 2 == 0:
+                stage(it + 1, rest // 2)
+
+        value_passes = []
+        for rows_sb, codes, scales in (
+            (h_sb[:], h_codes[:], h_scales[:]),
+            (w_sb[:, 0:QUAD, :], w_codes[:, :, 0:S], w_scales[:, :, 0:S]),
+            (w_sb[:, QUAD:H, :], w_codes[:, :, S : 2 * S], w_scales[:, :, S : 2 * S]),
+        ):
             for g in range(D_PASSES):
-                grouped = regroup_512_rows(flip_512_rows(rows_words, g, psum_e, "e"))
-                to_quantise.append((grouped, codes[:, g, :], scales[:, g, :]))
-                if len(to_quantise) > 1:
-                    quantise_512_rows(*to_quantise.pop(0))
-        head_factors()
-        for piece in range(4):
-            flip_qk(0, piece)
-            if piece == 0:
-                quantise_512_rows(*to_quantise.pop(0))
-            keep_qk(0, piece, on_vector=(piece % 2 == 0))
+                value_passes.append((rows_sb.bitcast(F32), g, codes[:, g, :], scales[:, g, :]))
+        value_tiles = {}
 
-        late_words, late_codes, late_scales = w_half(1)
-        late = {}
+        def flip_value(n):
+            rows_words, g, codes, scales = value_passes[n]
+            value_tiles[n] = flip_512_rows(rows_words, g)
 
-        def flip_late(g):
-            late[g] = flip_512_rows(late_words, g, psum_att, "att")
+        def regroup_value(n):
+            value_tiles[n] = regroup_512_rows(value_tiles[n])
 
-        def regroup_late(g):
-            late[g] = regroup_512_rows(late[g])
-
-        def quantise_late(g):
-            quantise_512_rows(late.pop(g), late_codes[:, g, :], late_scales[:, g, :])
+        def quantise_value(n):
+            rows_words, g, codes, scales = value_passes[n]
+            quantise_512_rows(value_tiles.pop(n), codes, scales)
 
         def pass_at(slot, lag, stage):
-            g = slot - lag
-            if 0 <= g < D_PASSES:
-                stage(g)
+            if 0 <= slot - lag < VALUE_PASSES:
+                stage(slot - lag)
 
-        for slot in range(LAG_ENERGY, UNITS + LAG_FINISH):
+        def heads_at(slot, lag, stage):
+            first = (slot - SLOT_PROJECT - lag) * PAIR
+            if 0 <= first < H:
+                stage(first)
+                stage(first + 1)
+
+        for piece in range(2):
+            flip_qk(0, piece)
+        for piece in range(2):
+            keep_qk(0, piece, on_vector=(piece == 0))
+
+        for slot in range(LAG_ENERGY, multiply_slot(PAIRS - 1) + LAG_FINISH + 1):
             unit_at(slot, LAG_ENERGY, energies)
-            head_at(slot, LAG_PROJECT, project)
-            pair_at(slot, LAG_MULTIPLY, multiply)
-            pass_at(slot, 1, flip_late)
+            if slot == LAG_ENERGY:
+                for piece in range(2, 4):
+                    flip_qk(0, piece)
+            heads_at(slot, 0, project)
+            for m in range(PAIRS):
+                if multiply_slot(m) == slot:
+                    multiply(m)
             pair_at(slot, LAG_FLIP, flip_scores)
-            piece_at(slot, 0, flip_qk)
+            piece_at(slot, 3, flip_qk)
+            pass_at(slot, SLOT_VALUE_PATH, flip_value)
             unit_at(slot, LAG_EXP, exponentials)
+            if slot == SLOT_FACTORS + 1:
+                factor_exps()
+                factor_bases()
+                factor_spread()
+            pass_at(slot, SLOT_VALUE_PATH + 1, regroup_value)
+            if slot == SLOT_FACTORS + 2:
+                factor_scales()
             unit_at(slot, LAG_RESCALE, rescale)
+            if slot == SLOT_FACTORS + 4:
+                factor_gains()
             unit_at(slot, LAG_JOIN, join)
-            pass_at(slot, 2, regroup_late)
-            head_at(slot, LAG_PROJECT + 1, regroup_v)
-            piece_at(slot, 1, keep_qk)
+            heads_at(slot, 1, regroup_v)
+            if slot == LAG_ENERGY + 1:
+                for piece in range(2, 4):
+                    keep_qk(0, piece, on_vector=(piece == 2))
+            piece_at(slot, 4, keep_qk)
             pair_at(slot, LAG_REGROUP, regroup_scores)
-            pair_at(slot, LAG_SQUARES, square_sums)
-            pass_at(slot, 3, quantise_late)
+            quad_at(slot, LAG_SQUARES, square_sums)
+            pass_at(slot, SLOT_VALUE_PATH + 2, quantise_value)
             for half in range(H // QUAD):
-                if slot == LAG_PROJECT + 1 + (half + 1) * QUAD:
+                if slot == SLOT_PROJECT + 1 + (half + 1) * 2:
                     quantise_v(half)
             pair_at(slot, LAG_QUANTISE, quantise_scores)
-            pair_at(slot, LAG_RMS, inverse_rms)
-            pair_at(slot, LAG_FINISH, finish)
+            quad_at(slot, LAG_RMS, inverse_rms)
+            quad_at(slot, LAG_FINISH, finish)
             unit_at(slot, LAG_ENERGY, maxima)
+            if slot == SLOT_FACTORS:
+                factor_dots()

@@ -33,19 +33,19 @@ MASKED = -1.0e30
 LAG_ENERGY = -1
 LAG_EXP = 0
 LAG_RESCALE = 1
-LAG_JOIN = 2
-LAG_FLIP = 4
-LAG_REGROUP = 5
-LAG_QUANTISE = 6
-LAG_MULTIPLY = 7
+LAG_JOIN = 3
+LAG_FLIP = 5
+LAG_REGROUP = 6
+LAG_QUANTISE = 8
+LAG_MULTIPLY = 9
 LAG_SQUARES = 1
 LAG_RMS = 2
 LAG_FINISH = 3
 VALUE_PASSES = 6
 SLOT_FACTORS = -1
 SLOT_VALUE_PATH = 0
-SLOT_PROJECT = 7
-SLOT_VALUES = 11
+SLOT_PROJECT = 6
+SLOT_VALUES = 14
 
 FLOPS = 2 * S * D * H * HD + 2 * H * C * S * S * HD + 2 * H * S * S * HD
 
@@ -95,18 +95,24 @@ def tile_attention_pb_kernel(
         warm = consts.tile([P, 1], F32, name="warm")
         nc.scalar.activation(out=warm[:], in_=neg_half[:, 0:1], func=ACT.Exp)
 
-        load_qk(0, slice(half_cols, 2 * half_cols))
         h_sb = loads.tile([P, ROW_TILES, D], BF16, name="h_sb")
         h_halves = h_sb[:].rearrange("p (u e) k -> p u (e k)", u=2)
         h_rows = h_norm.rearrange("b s k -> (b s) k").rearrange("(u p e) k -> p u (e k)", u=2, e=2)
         for u in range(2):
             nc.sync.dma_start(out=h_halves[:, u, :], in_=h_rows[:, u, :])
+        load_qk(0, slice(half_cols, 2 * half_cols))
         w_sb = loads.tile([P, H, D], BF16, name="w_sb")
         w_tiles = wv.rearrange("(o p) k -> p o k", p=P)
-        for first in range(0, H, PAIR):
-            heads = slice(first, first + PAIR)
-            nc.sync.dma_start(out=w_sb[:, heads, :], in_=w_tiles[:, heads, :])
-        for it in range(1, ROW_TILES):
+
+        def load_w(half):
+            for first in range(half * QUAD, (half + 1) * QUAD, PAIR):
+                heads = slice(first, first + PAIR)
+                nc.sync.dma_start(out=w_sb[:, heads, :], in_=w_tiles[:, heads, :])
+
+        load_w(0)
+        load_qk(1, slice(0, 2 * half_cols))
+        load_w(1)
+        for it in range(2, ROW_TILES):
             load_qk(it, slice(0, 2 * half_cols))
 
         sc_sb = keep.tile([P, H, S], BF16, name="sc_sb")
@@ -177,19 +183,19 @@ def tile_attention_pb_kernel(
                 op1=ALU.subtract,
             )
 
-        def factor_gains():
-            nc.gpsimd.tensor_scalar(
-                out=one_minus_lam[:], in0=lam_all, scalar1=-1.0, scalar2=1.0, op0=ALU.mult, op1=ALU.add
-            )
-            for h in range(H):
+        def factor_gain(h):
+            if h == 0:
                 nc.gpsimd.tensor_scalar(
-                    out=gain[:, h, :],
-                    in0=w_all,
-                    scalar1=one_minus_lam[:, h : h + 1],
-                    scalar2=0.0,
-                    op0=ALU.mult,
-                    op1=ALU.add,
+                    out=one_minus_lam[:], in0=lam_all, scalar1=-1.0, scalar2=1.0, op0=ALU.mult, op1=ALU.add
                 )
+            nc.gpsimd.tensor_scalar(
+                out=gain[:, h, :],
+                in0=w_all,
+                scalar1=one_minus_lam[:, h : h + 1],
+                scalar2=0.0,
+                op0=ALU.mult,
+                op1=ALU.add,
+            )
 
         qT = keep.tile([P, H * C, S], BF16, name="qT")
         kT = keep.tile([P, H * C, S], BF16, name="kT")
@@ -271,7 +277,7 @@ def tile_attention_pb_kernel(
 
         def regroup_v(h):
             v_bank = v_banks.pop(h)
-            if h % 2 == 0:
+            if h % 2 >= 0:
                 nc.vector.tensor_copy(out=v_grouped[:, h, :, :], in_=v_bank[:].rearrange("p t d -> p d t"))
             else:
                 nc.scalar.copy(out=v_grouped[:, h, :, :], in_=v_bank[:].rearrange("p t d -> p d t"))
@@ -293,28 +299,27 @@ def tile_attention_pb_kernel(
             if C * n <= S:
                 both = psum_e.tile([P, C, n], F32, name="e", tag="e")
                 energy = [both[:, c, :] for c in range(C)]
+                banks = [both[:]]
             else:
                 energy = [psum_e.tile([P, n], F32, name="e", tag="e")[:] for c in range(C)]
+                banks = energy
             for c in range(C):
                 hc = h * C + c
                 nc.tensor.matmul(energy[c], lhsT=qT[:, hc, rows], rhs=kT[:, hc, :n], start=True, stop=False)
                 nc.tensor.matmul(energy[c][:, rows], lhsT=ident_bf[:], rhs=mask_bf[:], start=False, stop=True)
-            unit_tiles[k] = {"energy": energy}
+            unit_tiles[k] = {"energy": energy, "banks": banks}
 
         def maxima(k):
-            n = (k // H + 1) * P
+            top = small.tile([P, C], F32, name="top")
+            banks = unit_tiles[k]["banks"]
+            per_bank = C // len(banks)
+            for n, bank in enumerate(banks):
+                nc.vector.reduce_max(out=top[:, n * per_bank : (n + 1) * per_bank], in_=bank, axis=AX.X)
+            unit_tiles[k]["top"] = top
+
+        def shifts(k):
             shift = small.tile([P, C], F32, name="shift")
-            for c in range(C):
-                neg_scaled = work.tile([P, S], BF16, name="neg_scaled", bufs=3)
-                nc.vector.tensor_scalar(
-                    out=neg_scaled[:, :n],
-                    in0=unit_tiles[k]["energy"][c],
-                    scalar1=-SM_SCALE,
-                    scalar2=None,
-                    op0=ALU.mult,
-                    op1=ALU.min,
-                    accum_out=shift[:, c : c + 1],
-                )
+            nc.scalar.activation(out=shift[:], in_=unit_tiles[k]["top"][:], func=ACT.Copy, scale=-SM_SCALE)
             unit_tiles[k]["shift"] = shift
 
         def exponentials(k):
@@ -322,7 +327,7 @@ def tile_attention_pb_kernel(
             sums = small.tile([P, C], F32, name="sums")
             probs = []
             for c in range(C):
-                p = work.tile([P, S], F32, name="p%d" % c, bufs=4)
+                p = work.tile([P, S], F32, name="p%d" % c, bufs=5)
                 nc.scalar.activation(
                     out=p[:, :n],
                     in_=unit_tiles[k]["energy"][c],
@@ -382,8 +387,8 @@ def tile_attention_pb_kernel(
             pair_tiles[m]["grouped"] = sc_grouped
 
         def quantise_scores(m):
-            sc_codes = work.tile([P, PAIR * P], U32, name="sc_codes", bufs=4, align_bytes=64)
-            sc_scales = work.tile([P, PAIR * P], U8, name="sc_scales", bufs=4, align_bytes=64)
+            sc_codes = work.tile([P, PAIR * P], U32, name="sc_codes", bufs=6, align_bytes=64)
+            sc_scales = work.tile([P, PAIR * P], U8, name="sc_scales", bufs=6, align_bytes=64)
             nc.vector.quantize_mx(
                 out=sc_codes[:].bitcast(FP8X4),
                 scales=sc_scales[:],
@@ -423,7 +428,7 @@ def tile_attention_pb_kernel(
                 )
             quad_tiles[quad]["sum_sq"] = sum_sq
 
-        def inverse_rms(quad):
+        def mean_squares(quad):
             mean_sq = small.tile([P, QUAD], F32, name="mean_sq")
             nc.gpsimd.tensor_scalar(
                 out=mean_sq[:],
@@ -433,8 +438,13 @@ def tile_attention_pb_kernel(
                 op0=ALU.mult,
                 op1=ALU.add,
             )
+            quad_tiles[quad]["mean_sq"] = mean_sq
+
+        def inverse_rms(quad):
             rstd = small.tile([P, QUAD], F32, name="rstd")
-            nc.gpsimd.tensor_tensor(out=rstd[:], in0=mean_sq[:], in1=neg_half[:], op=ALU.pow)
+            nc.gpsimd.tensor_tensor(
+                out=rstd[:], in0=quad_tiles[quad]["mean_sq"][:], in1=neg_half[:], op=ALU.pow
+            )
             quad_tiles[quad]["rstd"] = rstd
 
         def finish(quad):
@@ -503,29 +513,33 @@ def tile_attention_pb_kernel(
             if 0 <= slot - lag < VALUE_PASSES:
                 stage(slot - lag)
 
-        def heads_at(slot, lag, stage):
-            first = (slot - SLOT_PROJECT - lag) * PAIR
-            if 0 <= first < H:
-                stage(first)
-                stage(first + 1)
+        def head_at(slot, lag, stage):
+            h = slot - SLOT_PROJECT - lag
+            if 0 <= h < H:
+                stage(h)
 
         for piece in range(2):
             flip_qk(0, piece)
         for piece in range(2):
             keep_qk(0, piece, on_vector=(piece == 0))
 
+        factor_dots()
+
         for slot in range(LAG_ENERGY, multiply_slot(PAIRS - 1) + LAG_FINISH + 1):
             unit_at(slot, LAG_ENERGY, energies)
-            if slot == LAG_ENERGY:
+            if slot == 0:
                 for piece in range(2, 4):
                     flip_qk(0, piece)
-            heads_at(slot, 0, project)
+            head_at(slot, 0, project)
             for m in range(PAIRS):
                 if multiply_slot(m) == slot:
                     multiply(m)
             pair_at(slot, LAG_FLIP, flip_scores)
-            piece_at(slot, 3, flip_qk)
+            piece_at(slot, 2, flip_qk)
             pass_at(slot, SLOT_VALUE_PATH, flip_value)
+            unit_at(slot, LAG_EXP, shifts)
+            piece_at(slot, 3, keep_qk)
+            pair_at(slot, LAG_REGROUP, regroup_scores)
             unit_at(slot, LAG_EXP, exponentials)
             if slot == SLOT_FACTORS + 1:
                 factor_exps()
@@ -534,24 +548,20 @@ def tile_attention_pb_kernel(
             pass_at(slot, SLOT_VALUE_PATH + 1, regroup_value)
             if slot == SLOT_FACTORS + 2:
                 factor_scales()
-            unit_at(slot, LAG_RESCALE, rescale)
-            if slot == SLOT_FACTORS + 4:
-                factor_gains()
             unit_at(slot, LAG_JOIN, join)
-            heads_at(slot, 1, regroup_v)
-            if slot == LAG_ENERGY + 1:
+            head_at(slot, 1, regroup_v)
+            if slot == 1:
                 for piece in range(2, 4):
                     keep_qk(0, piece, on_vector=(piece == 2))
-            piece_at(slot, 4, keep_qk)
-            pair_at(slot, LAG_REGROUP, regroup_scores)
             quad_at(slot, LAG_SQUARES, square_sums)
             pass_at(slot, SLOT_VALUE_PATH + 2, quantise_value)
             for half in range(H // QUAD):
-                if slot == SLOT_PROJECT + 1 + (half + 1) * 2:
+                if slot == SLOT_PROJECT + 1 + (half + 1) * QUAD:
                     quantise_v(half)
             pair_at(slot, LAG_QUANTISE, quantise_scores)
+            quad_at(slot, LAG_RMS, mean_squares)
+            unit_at(slot, LAG_RESCALE, rescale)
+            head_at(slot, 0, factor_gain)
             quad_at(slot, LAG_RMS, inverse_rms)
-            quad_at(slot, LAG_FINISH, finish)
             unit_at(slot, LAG_ENERGY, maxima)
-            if slot == SLOT_FACTORS:
-                factor_dots()
+            quad_at(slot, LAG_FINISH, finish)

@@ -25,7 +25,7 @@ QUAD = 4
 PAIR = 2
 UNITS = ROW_TILES * H
 PAIRS = UNITS // PAIR
-QUADS = UNITS // QUAD
+GROUPS = [(2 * q, 2 * q + 1) for q in range(PAIRS // 2 - 1)] + [(PAIRS - 2,), (PAIRS - 1,)]
 SM_SCALE = 1.0 / (HD ** 0.5)
 EPS = 1e-9
 MASKED = -1.0e30
@@ -83,8 +83,9 @@ def tile_attention_pb_kernel(
             nc.sync.dma_start(out=q_sb[it][:, cols], in_=q_rows[rows, cols])
             nc.sync.dma_start(out=k_sb[it][:, cols], in_=k_rows[rows, cols])
 
-        half_cols = H * C * HD // 2
-        load_qk(0, slice(0, half_cols))
+        quarter = H * C * HD // 4
+        load_qk(0, slice(0, quarter))
+        load_qk(0, slice(quarter, 2 * quarter))
 
         qk_vec = consts.tile([H, 4, HD], BF16, name="qk_vec")
         for n, vec in enumerate((q1, q2, k1, k2)):
@@ -100,7 +101,7 @@ def tile_attention_pb_kernel(
         h_rows = h_norm.rearrange("b s k -> (b s) k").rearrange("(u p e) k -> p u (e k)", u=2, e=2)
         for u in range(2):
             nc.sync.dma_start(out=h_halves[:, u, :], in_=h_rows[:, u, :])
-        load_qk(0, slice(half_cols, 2 * half_cols))
+        load_qk(0, slice(2 * quarter, 4 * quarter))
         w_sb = loads.tile([P, H, D], BF16, name="w_sb")
         w_tiles = wv.rearrange("(o p) k -> p o k", p=P)
 
@@ -110,10 +111,10 @@ def tile_attention_pb_kernel(
                 nc.sync.dma_start(out=w_sb[:, heads, :], in_=w_tiles[:, heads, :])
 
         load_w(0)
-        load_qk(1, slice(0, 2 * half_cols))
+        load_qk(1, slice(0, 4 * quarter))
         load_w(1)
         for it in range(2, ROW_TILES):
-            load_qk(it, slice(0, 2 * half_cols))
+            load_qk(it, slice(0, 4 * quarter))
 
         sc_sb = keep.tile([P, H, S], BF16, name="sc_sb")
         nc.vector.memset(sc_sb[:].rearrange("p h s -> p (h s)").bitcast(U32), 0)
@@ -135,6 +136,8 @@ def tile_attention_pb_kernel(
         make_identity(nc, ident_f32[:], nomemset=True)
         ones_bf = consts.tile([P, P], BF16, name="ones_bf")
         nc.vector.memset(ones_bf[:], 1.0)
+        eps = consts.tile([P, 1], F32, name="eps")
+        nc.vector.memset(eps[:], EPS)
         base = consts.tile([P, 1], F32, name="base")
         nc.vector.memset(base[:], 0.0)
 
@@ -200,22 +203,34 @@ def tile_attention_pb_kernel(
         qT = keep.tile([P, H * C, S], BF16, name="qT")
         kT = keep.tile([P, H * C, S], BF16, name="kT")
 
+        def qk_piece(which, it, first, heads):
+            return (q_sb, k_sb)[which][it], (qT, kT)[which], it, first * C, heads * C
+
+        pieces = [
+            (-2, qk_piece(0, 0, 0, 2)),
+            (-2, qk_piece(1, 0, 0, 2)),
+            (-1, qk_piece(0, 0, 2, 2)),
+            (-1, qk_piece(1, 0, 2, 2)),
+            (0, qk_piece(0, 0, 4, 4)),
+            (1, qk_piece(1, 0, 4, 4)),
+        ]
+        for it in range(1, ROW_TILES):
+            for n in range(4):
+                pieces.append(((it - 1) * H + 2 + 2 * n, qk_piece(n % 2, it, n // 2 * 4, 4)))
         qk_banks = {}
 
-        def flip_qk(it, piece):
-            rows_sb = (q_sb[it], k_sb[it])[piece % 2]
-            first = (piece // 2) * QUAD * C
-            bank = psum_t.tile([P, QUAD * C, P], BF16, name="qk_bank", tag="t")
-            for n in range(QUAD * C):
+        def flip_qk(piece):
+            rows_sb, flipped, it, first, count = pieces[piece][1]
+            bank = psum_t.tile([P, count, P], BF16, name="qk_bank", tag="t")
+            for n in range(count):
                 hc = first + n
                 nc.tensor.transpose(bank[:, n, :], rows_sb[:, hc * HD : (hc + 1) * HD], ident_bf[:])
-            qk_banks[(it, piece)] = bank
+            qk_banks[piece] = bank
 
-        def keep_qk(it, piece, on_vector=False):
-            flipped = (qT, kT)[piece % 2]
-            first = (piece // 2) * QUAD * C
-            kept = flipped[:, first : first + QUAD * C, it * P : (it + 1) * P]
-            bank = qk_banks.pop((it, piece))
+        def keep_qk(piece, on_vector=False):
+            rows_sb, flipped, it, first, count = pieces[piece][1]
+            kept = flipped[:, first : first + count, it * P : (it + 1) * P]
+            bank = qk_banks.pop(piece)
             if on_vector:
                 nc.vector.tensor_copy(out=kept, in_=bank[:])
             else:
@@ -346,7 +361,8 @@ def tile_attention_pb_kernel(
             recip = small.tile([P, C], F32, name="recip")
             nc.vector.reciprocal(out=recip[:], in_=unit_tiles[k]["sums"][:])
             p1 = unit_tiles[k]["probs"][1]
-            nc.gpsimd.tensor_scalar(
+            engine = nc.vector if k >= UNITS - PAIR else nc.gpsimd
+            engine.tensor_scalar(
                 out=p1[:, :n],
                 in0=p1[:, :n],
                 scalar1=recip[:, 1:2],
@@ -371,6 +387,8 @@ def tile_attention_pb_kernel(
 
         pair_tiles = {}
         quad_tiles = {}
+        late_quads = range(len(GROUPS) - 4, len(GROUPS))
+        group_of = {m: g for g, pairs in enumerate(GROUPS) for m in pairs}
         out_rows = out.rearrange("b s h d -> (b s) (h d)")
 
         def flip_scores(m):
@@ -399,9 +417,11 @@ def tile_attention_pb_kernel(
 
         def multiply(m):
             first = (m * PAIR) % H
-            quad, second = divmod(m, 2)
+            quad = group_of[m]
+            second = GROUPS[quad].index(m)
             if not second:
-                quad_tiles[quad] = {"att": psum_att.tile([P, QUAD, HD], F32, name="att", tag="att")}
+                pool, tag = (psum_e, "e") if m == PAIRS - 1 else (psum_att, "att")
+                quad_tiles[quad] = {"att": pool.tile([P, QUAD, HD], F32, name="att", tag=tag)}
             tiles = pair_tiles.pop(m)
             for r in range(PAIR):
                 i_cols = slice(r * P, (r + 1) * P)
@@ -419,20 +439,23 @@ def tile_attention_pb_kernel(
         def square_sums(quad):
             squares = work.tile([P, QUAD, HD], BF16, name="squares")
             sum_sq = small.tile([P, QUAD], F32, name="sum_sq")
-            for r in range(QUAD):
+            heads = PAIR * len(GROUPS[quad])
+            for r in range(heads):
                 nc.scalar.activation(
                     out=squares[:, r, :],
                     in_=quad_tiles[quad]["att"][:, r, :],
                     func=ACT.Square,
                     accum_out=sum_sq[:, r : r + 1],
                 )
-            quad_tiles[quad]["sum_sq"] = sum_sq
+            quad_tiles[quad]["sum_sq"] = sum_sq[:, 0:heads]
 
         def mean_squares(quad):
+            if quad in late_quads:
+                return
             mean_sq = small.tile([P, QUAD], F32, name="mean_sq")
             nc.gpsimd.tensor_scalar(
                 out=mean_sq[:],
-                in0=quad_tiles[quad]["sum_sq"][:],
+                in0=quad_tiles[quad]["sum_sq"],
                 scalar1=1.0 / HD,
                 scalar2=EPS,
                 op0=ALU.mult,
@@ -442,16 +465,27 @@ def tile_attention_pb_kernel(
 
         def inverse_rms(quad):
             rstd = small.tile([P, QUAD], F32, name="rstd")
+            quad_tiles[quad]["rstd"] = rstd
+            heads = PAIR * len(GROUPS[quad])
+            if quad in late_quads:
+                root = small.tile([P, QUAD], F32, name="root")
+                nc.scalar.activation(
+                    out=root[:, 0:heads], in_=quad_tiles[quad]["sum_sq"], func=ACT.Sqrt, bias=eps[:, 0:1], scale=1.0 / HD
+                )
+                quad_tiles[quad]["root"] = root
+                return
             nc.gpsimd.tensor_tensor(
                 out=rstd[:], in0=quad_tiles[quad]["mean_sq"][:], in1=neg_half[:], op=ALU.pow
             )
-            quad_tiles[quad]["rstd"] = rstd
 
         def finish(quad):
-            it, first = divmod(quad * QUAD, H)
+            it, first = divmod(GROUPS[quad][0] * PAIR, H)
+            heads = PAIR * len(GROUPS[quad])
             tiles = quad_tiles.pop(quad)
             normed = work.tile([P, QUAD, HD], F32, name="normed", bufs=3)
-            for r in range(QUAD):
+            if quad in late_quads:
+                nc.vector.reciprocal(out=tiles["rstd"][:, 0:heads], in_=tiles["root"][:, 0:heads])
+            for r in range(heads):
                 nc.vector.scalar_tensor_tensor(
                     out=normed[:, r, :],
                     in0=tiles["att"][:, r, :],
@@ -461,8 +495,8 @@ def tile_attention_pb_kernel(
                     op1=ALU.mult,
                 )
             nc.sync.dma_start(
-                out=out_rows[it * P : (it + 1) * P, first * HD : (first + QUAD) * HD],
-                in_=normed[:].rearrange("p r d -> p (r d)"),
+                out=out_rows[it * P : (it + 1) * P, first * HD : (first + heads) * HD],
+                in_=normed[:, 0:heads, :].rearrange("p r d -> p (r d)"),
             )
 
         def unit_at(slot, lag, stage):
@@ -476,17 +510,17 @@ def tile_attention_pb_kernel(
                 stage(m)
 
         def multiply_slot(m):
-            return max(2 * m + LAG_MULTIPLY, SLOT_VALUES + m)
+            return max(2 * m + LAG_MULTIPLY, SLOT_VALUES + m + 2 * (m >= QUAD))
 
         def quad_at(slot, lag, stage):
-            for quad in range(QUADS):
-                if multiply_slot(2 * quad + 1) + lag == slot:
+            for quad in range(len(GROUPS)):
+                if multiply_slot(GROUPS[quad][-1]) + lag == slot:
                     stage(quad)
 
         def piece_at(slot, lag, stage):
-            it, rest = divmod(slot - lag, H)
-            if 0 <= it < ROW_TILES - 1 and rest % 2 == 0:
-                stage(it + 1, rest // 2)
+            for piece in range(len(pieces)):
+                if pieces[piece][0] + lag == slot:
+                    stage(piece)
 
         value_passes = []
         for rows_sb, codes, scales in (
@@ -518,41 +552,30 @@ def tile_attention_pb_kernel(
             if 0 <= h < H:
                 stage(h)
 
-        for piece in range(2):
-            flip_qk(0, piece)
-        for piece in range(2):
-            keep_qk(0, piece, on_vector=(piece == 0))
-
+        flip_qk(0)
+        flip_qk(1)
+        keep_qk(0, on_vector=True)
+        keep_qk(1)
         factor_dots()
+        factor_exps()
 
-        for slot in range(LAG_ENERGY, multiply_slot(PAIRS - 1) + LAG_FINISH + 1):
+        for slot in range(LAG_ENERGY, UNITS):
             unit_at(slot, LAG_ENERGY, energies)
-            if slot == 0:
-                for piece in range(2, 4):
-                    flip_qk(0, piece)
+            pair_at(slot, LAG_FLIP, flip_scores)
             head_at(slot, 0, project)
             for m in range(PAIRS):
                 if multiply_slot(m) == slot:
                     multiply(m)
-            pair_at(slot, LAG_FLIP, flip_scores)
-            piece_at(slot, 2, flip_qk)
             pass_at(slot, SLOT_VALUE_PATH, flip_value)
+            piece_at(slot, 0, flip_qk)
             unit_at(slot, LAG_EXP, shifts)
-            piece_at(slot, 3, keep_qk)
+            pass_at(slot, SLOT_VALUE_PATH + 1, regroup_value)
+            if slot > LAG_ENERGY:
+                piece_at(slot, 1, keep_qk)
             pair_at(slot, LAG_REGROUP, regroup_scores)
             unit_at(slot, LAG_EXP, exponentials)
-            if slot == SLOT_FACTORS + 1:
-                factor_exps()
-                factor_bases()
-                factor_spread()
-            pass_at(slot, SLOT_VALUE_PATH + 1, regroup_value)
-            if slot == SLOT_FACTORS + 2:
-                factor_scales()
-            unit_at(slot, LAG_JOIN, join)
             head_at(slot, 1, regroup_v)
-            if slot == 1:
-                for piece in range(2, 4):
-                    keep_qk(0, piece, on_vector=(piece == 2))
+            unit_at(slot, LAG_JOIN, join)
             quad_at(slot, LAG_SQUARES, square_sums)
             pass_at(slot, SLOT_VALUE_PATH + 2, quantise_value)
             for half in range(H // QUAD):
@@ -560,8 +583,44 @@ def tile_attention_pb_kernel(
                     quantise_v(half)
             pair_at(slot, LAG_QUANTISE, quantise_scores)
             quad_at(slot, LAG_RMS, mean_squares)
+            if slot == SLOT_FACTORS + 2:
+                factor_scales()
             unit_at(slot, LAG_RESCALE, rescale)
             head_at(slot, 0, factor_gain)
             quad_at(slot, LAG_RMS, inverse_rms)
             unit_at(slot, LAG_ENERGY, maxima)
+            if slot == SLOT_FACTORS + 1:
+                factor_bases()
+                factor_spread()
             quad_at(slot, LAG_FINISH, finish)
+
+        square_sums(5)
+        regroup_scores(13)
+        nc.scalar.activation(out=warm[:], in_=eps[:], func=ACT.Sqrt)
+        quantise_scores(12)
+        join(29)
+        multiply(12)
+        flip_scores(14)
+        inverse_rms(5)
+        regroup_scores(14)
+        rescale(31)
+        join(30)
+        join(31)
+        flip_scores(15)
+        regroup_scores(15)
+        quantise_scores(13)
+        multiply(13)
+        finish(5)
+        square_sums(6)
+        quantise_scores(14)
+        multiply(14)
+        square_sums(7)
+        inverse_rms(6)
+        quantise_scores(15)
+        multiply(15)
+        square_sums(8)
+        finish(6)
+        inverse_rms(7)
+        inverse_rms(8)
+        finish(7)
+        finish(8)

@@ -39,8 +39,7 @@ LAG_REGROUP = 6
 LAG_QUANTISE = 8
 LAG_MULTIPLY = 9
 LAG_SQUARES = 1
-LAG_RMS = 2
-LAG_FINISH = 3
+LAG_WEIGH = 2
 VALUE_PASSES = 6
 SLOT_FACTORS = -1
 SLOT_VALUE_PATH = 0
@@ -387,6 +386,10 @@ def tile_attention_pb_kernel(
 
         pair_tiles = {}
         quad_tiles = {}
+        sum_all = keep.tile([P, 5 * QUAD], F32, name="sum_all")
+        root_all = keep.tile([P, 5 * QUAD], F32, name="root_all")
+        rstd_all = keep.tile([P, 5 * QUAD], F32, name="rstd_all")
+        weighed = keep.tile([P, 5 * QUAD, HD], F32, name="weighed")
         late_quads = range(len(GROUPS) - 4, len(GROUPS))
         group_of = {m: g for g, pairs in enumerate(GROUPS) for m in pairs}
         out_rows = out.rearrange("b s h d -> (b s) (h d)")
@@ -420,7 +423,7 @@ def tile_attention_pb_kernel(
             quad = group_of[m]
             second = GROUPS[quad].index(m)
             if not second:
-                pool, tag = (psum_e, "e") if m == PAIRS - 1 else (psum_att, "att")
+                pool, tag = (psum_e, "e") if m >= PAIRS - 2 else (psum_att, "att")
                 quad_tiles[quad] = {"att": pool.tile([P, QUAD, HD], F32, name="att", tag=tag)}
             tiles = pair_tiles.pop(m)
             for r in range(PAIR):
@@ -438,8 +441,11 @@ def tile_attention_pb_kernel(
 
         def square_sums(quad):
             squares = work.tile([P, QUAD, HD], BF16, name="squares")
-            sum_sq = small.tile([P, QUAD], F32, name="sum_sq")
             heads = PAIR * len(GROUPS[quad])
+            if quad in late_quads:
+                sum_sq = small.tile([P, QUAD], F32, name="sum_sq")
+            else:
+                sum_sq = sum_all[:, quad * QUAD : (quad + 1) * QUAD]
             for r in range(heads):
                 nc.scalar.activation(
                     out=squares[:, r, :],
@@ -449,47 +455,59 @@ def tile_attention_pb_kernel(
                 )
             quad_tiles[quad]["sum_sq"] = sum_sq[:, 0:heads]
 
-        def mean_squares(quad):
-            if quad in late_quads:
-                return
-            mean_sq = small.tile([P, QUAD], F32, name="mean_sq")
-            nc.gpsimd.tensor_scalar(
-                out=mean_sq[:],
-                in0=quad_tiles[quad]["sum_sq"],
-                scalar1=1.0 / HD,
-                scalar2=EPS,
-                op0=ALU.mult,
-                op1=ALU.add,
+        def weigh(quad):
+            it, first = divmod(quad * QUAD, H)
+            nc.vector.tensor_tensor(
+                out=weighed[:, quad * QUAD : (quad + 1) * QUAD, :],
+                in0=quad_tiles.pop(quad)["att"][:],
+                in1=gain[:, first : first + QUAD, :],
+                op=ALU.mult,
             )
-            quad_tiles[quad]["mean_sq"] = mean_sq
 
-        def inverse_rms(quad):
-            rstd = small.tile([P, QUAD], F32, name="rstd")
-            quad_tiles[quad]["rstd"] = rstd
+        def roots(quad):
+            root = small.tile([P, QUAD], F32, name="root")
             heads = PAIR * len(GROUPS[quad])
-            if quad in late_quads:
-                root = small.tile([P, QUAD], F32, name="root")
-                nc.scalar.activation(
-                    out=root[:, 0:heads], in_=quad_tiles[quad]["sum_sq"], func=ACT.Sqrt, bias=eps[:, 0:1], scale=1.0 / HD
+            nc.scalar.activation(
+                out=root[:, 0:heads], in_=quad_tiles[quad]["sum_sq"], func=ACT.Sqrt, bias=eps[:, 0:1], scale=1.0 / HD
+            )
+            quad_tiles[quad]["root"] = root
+
+        def early_roots():
+            nc.scalar.activation(out=root_all[:], in_=sum_all[:], func=ACT.Sqrt, bias=eps[:, 0:1], scale=1.0 / HD)
+
+        def early_rms():
+            nc.vector.reciprocal(out=rstd_all[:], in_=root_all[:])
+
+        def divide(quad, engine=nc.gpsimd):
+            it, first = divmod(quad * QUAD, H)
+            rows = weighed[:, quad * QUAD : (quad + 1) * QUAD, :]
+            for r in range(QUAD):
+                n = quad * QUAD + r
+                engine.tensor_scalar(
+                    out=weighed[:, n, :],
+                    in0=weighed[:, n, :],
+                    scalar1=rstd_all[:, n : n + 1],
+                    scalar2=0.0,
+                    op0=ALU.mult,
+                    op1=ALU.add,
                 )
-                quad_tiles[quad]["root"] = root
-                return
-            nc.gpsimd.tensor_tensor(
-                out=rstd[:], in0=quad_tiles[quad]["mean_sq"][:], in1=neg_half[:], op=ALU.pow
+            nc.sync.dma_start(
+                out=out_rows[it * P : (it + 1) * P, first * HD : (first + QUAD) * HD],
+                in_=rows.rearrange("p r d -> p (r d)"),
             )
 
         def finish(quad):
             it, first = divmod(GROUPS[quad][0] * PAIR, H)
             heads = PAIR * len(GROUPS[quad])
             tiles = quad_tiles.pop(quad)
-            normed = work.tile([P, QUAD, HD], F32, name="normed", bufs=3)
-            if quad in late_quads:
-                nc.vector.reciprocal(out=tiles["rstd"][:, 0:heads], in_=tiles["root"][:, 0:heads])
+            normed = work.tile([P, QUAD, HD], F32, name="normed", bufs=4)
+            rstd = small.tile([P, QUAD], F32, name="rstd")
+            nc.vector.reciprocal(out=rstd[:, 0:heads], in_=tiles["root"][:, 0:heads])
             for r in range(heads):
                 nc.vector.scalar_tensor_tensor(
                     out=normed[:, r, :],
                     in0=tiles["att"][:, r, :],
-                    scalar=tiles["rstd"][:, r : r + 1],
+                    scalar=rstd[:, r : r + 1],
                     in1=gain[:, first + r, :],
                     op0=ALU.mult,
                     op1=ALU.mult,
@@ -510,7 +528,7 @@ def tile_attention_pb_kernel(
                 stage(m)
 
         def multiply_slot(m):
-            return max(2 * m + LAG_MULTIPLY, SLOT_VALUES + m + 2 * (m >= QUAD))
+            return max(2 * m + LAG_MULTIPLY, SLOT_VALUES + m + (m >= QUAD))
 
         def quad_at(slot, lag, stage):
             for quad in range(len(GROUPS)):
@@ -582,45 +600,47 @@ def tile_attention_pb_kernel(
                 if slot == SLOT_PROJECT + 1 + (half + 1) * QUAD:
                     quantise_v(half)
             pair_at(slot, LAG_QUANTISE, quantise_scores)
-            quad_at(slot, LAG_RMS, mean_squares)
             if slot == SLOT_FACTORS + 2:
                 factor_scales()
             unit_at(slot, LAG_RESCALE, rescale)
             head_at(slot, 0, factor_gain)
-            quad_at(slot, LAG_RMS, inverse_rms)
             unit_at(slot, LAG_ENERGY, maxima)
             if slot == SLOT_FACTORS + 1:
                 factor_bases()
                 factor_spread()
-            quad_at(slot, LAG_FINISH, finish)
+            quad_at(slot, LAG_WEIGH, weigh)
 
-        square_sums(5)
-        regroup_scores(13)
         nc.scalar.activation(out=warm[:], in_=eps[:], func=ACT.Sqrt)
+        early_roots()
         quantise_scores(12)
         join(29)
         multiply(12)
         flip_scores(14)
-        inverse_rms(5)
-        regroup_scores(14)
         rescale(31)
+        regroup_scores(13)
         join(30)
         join(31)
+        early_rms()
+        for quad in range(5):
+            divide(quad)
+        square_sums(5)
+        regroup_scores(14)
         flip_scores(15)
+        roots(5)
         regroup_scores(15)
         quantise_scores(13)
         multiply(13)
-        finish(5)
-        square_sums(6)
         quantise_scores(14)
         multiply(14)
+        square_sums(6)
         square_sums(7)
-        inverse_rms(6)
+        roots(6)
         quantise_scores(15)
         multiply(15)
         square_sums(8)
+        finish(5)
         finish(6)
-        inverse_rms(7)
-        inverse_rms(8)
+        roots(7)
+        roots(8)
         finish(7)
         finish(8)

@@ -86,12 +86,6 @@ def tile_attention_pb_kernel(
         load_qk(0, slice(0, quarter))
         load_qk(0, slice(quarter, 2 * quarter))
 
-        qk_vec = consts.tile([H, 4, HD], BF16, name="qk_vec")
-        for n, vec in enumerate((q1, q2, k1, k2)):
-            nc.scalar.dma_start(out=qk_vec[:, n, :], in_=vec.rearrange("h d o -> h (d o)"))
-        nc.scalar.dma_start(out=row0[0:1, 0:HD], in_=head_norm_w.rearrange("(o d) -> o d", o=1))
-        nc.scalar.dma_start(out=row0[0:1, P : P + H], in_=lam_init.rearrange("(o h) -> o h", o=1))
-
         warm = consts.tile([P, 1], F32, name="warm")
         nc.scalar.activation(out=warm[:], in_=neg_half[:, 0:1], func=ACT.Exp)
 
@@ -100,6 +94,11 @@ def tile_attention_pb_kernel(
         h_rows = h_norm.rearrange("b s k -> (b s) k").rearrange("(u p e) k -> p u (e k)", u=2, e=2)
         for u in range(2):
             nc.sync.dma_start(out=h_halves[:, u, :], in_=h_rows[:, u, :])
+        qk_vec = consts.tile([H, 4, HD], BF16, name="qk_vec")
+        for n, vec in enumerate((q1, q2, k1, k2)):
+            nc.scalar.dma_start(out=qk_vec[:, n, :], in_=vec.rearrange("h d o -> h (d o)"))
+        nc.scalar.dma_start(out=row0[0:1, 0:HD], in_=head_norm_w.rearrange("(o d) -> o d", o=1))
+        nc.scalar.dma_start(out=row0[0:1, P : P + H], in_=lam_init.rearrange("(o h) -> o h", o=1))
         load_qk(0, slice(2 * quarter, 4 * quarter))
         w_sb = loads.tile([P, H, D], BF16, name="w_sb")
         w_tiles = wv.rearrange("(o p) k -> p o k", p=P)
@@ -110,13 +109,11 @@ def tile_attention_pb_kernel(
                 nc.sync.dma_start(out=w_sb[:, heads, :], in_=w_tiles[:, heads, :])
 
         load_w(0)
-        load_qk(1, slice(0, 4 * quarter))
         load_w(1)
+        load_qk(1, slice(0, 4 * quarter))
         for it in range(2, ROW_TILES):
             load_qk(it, slice(0, 4 * quarter))
 
-        sc_sb = keep.tile([P, H, S], BF16, name="sc_sb")
-        nc.vector.memset(sc_sb[:].rearrange("p h s -> p (h s)").bitcast(U32), 0)
         mask_f32 = consts.tile([P, P], F32, name="mask_f32")
         nc.vector.memset(mask_f32[:], 0.0)
         nc.gpsimd.affine_select(
@@ -128,8 +125,6 @@ def tile_attention_pb_kernel(
             pattern=[[-1, P]],
             channel_multiplier=1,
         )
-        mask_bf = consts.tile([P, P], BF16, name="mask_bf")
-        nc.vector.tensor_copy(out=mask_bf[:], in_=mask_f32[:])
         ident_f32 = consts.tile([P, P], F32, name="ident_f32")
         nc.vector.memset(ident_f32[:], 0.0)
         make_identity(nc, ident_f32[:], nomemset=True)
@@ -139,6 +134,10 @@ def tile_attention_pb_kernel(
         nc.vector.memset(eps[:], EPS)
         base = consts.tile([P, 1], F32, name="base")
         nc.vector.memset(base[:], 0.0)
+        sc_sb = keep.tile([P, H, S], BF16, name="sc_sb")
+        nc.vector.memset(sc_sb[:].rearrange("p h s -> p (h s)").bitcast(U32), 0)
+        mask_bf = consts.tile([P, P], BF16, name="mask_bf")
+        nc.vector.tensor_copy(out=mask_bf[:], in_=mask_f32[:])
 
         scale_all = consts.tile([P, H], F32, name="scale_all")
         gain = consts.tile([P, H, HD], F32, name="gain")
@@ -163,12 +162,12 @@ def tile_attention_pb_kernel(
             nc.vector.tensor_sub(out=base[0:H, :], in0=exps[:, 0:1], in1=exps[:, 1:2])
 
         def factor_spread():
-            base_all = psum_att.tile([P, P], F32, name="base_all", tag="att")
+            bank = psum_e.tile([P, 3, P], F32, name="factor_bank", tag="e")
+            base_all, row_bank = bank[:, 0, :], bank[:, 1:3, :].rearrange("p a c -> p (a c)")
             nc.tensor.matmul(
-                base_all[:], lhsT=base[:, 0:1].to_broadcast([P, P]), rhs=ident_f32[:], start=True, stop=True
+                base_all, lhsT=base[:, 0:1].to_broadcast([P, P]), rhs=ident_f32[:], start=True, stop=True
             )
-            row_bank = psum_att.tile([P, 2 * P], F32, name="row_bank", tag="att")
-            nc.tensor.matmul(row_bank[:], lhsT=ones_bf[:], rhs=row0[:], start=True, stop=True)
+            nc.tensor.matmul(row_bank, lhsT=ones_bf[:], rhs=row0[:], start=True, stop=True)
             factor_banks["base"] = base_all
             factor_banks["row"] = row_bank
 
@@ -215,7 +214,7 @@ def tile_attention_pb_kernel(
         ]
         for it in range(1, ROW_TILES):
             for n in range(4):
-                pieces.append(((it - 1) * H + 2 + 2 * n, qk_piece(n % 2, it, n // 2 * 4, 4)))
+                pieces.append(((it - 1) * H + ((4, 5, 6, 8) if it == 1 else (2, 4, 6, 8))[n], qk_piece(n % 2, it, n // 2 * 4, 4)))
         qk_banks = {}
 
         def flip_qk(piece):
@@ -574,8 +573,6 @@ def tile_attention_pb_kernel(
         flip_qk(1)
         keep_qk(0, on_vector=True)
         keep_qk(1)
-        factor_dots()
-        factor_exps()
 
         for slot in range(LAG_ENERGY, UNITS):
             unit_at(slot, LAG_ENERGY, energies)
@@ -585,13 +582,14 @@ def tile_attention_pb_kernel(
                 if multiply_slot(m) == slot:
                     multiply(m)
             pass_at(slot, SLOT_VALUE_PATH, flip_value)
-            piece_at(slot, 0, flip_qk)
             unit_at(slot, LAG_EXP, shifts)
             pass_at(slot, SLOT_VALUE_PATH + 1, regroup_value)
             if slot > LAG_ENERGY:
                 piece_at(slot, 1, keep_qk)
             pair_at(slot, LAG_REGROUP, regroup_scores)
             unit_at(slot, LAG_EXP, exponentials)
+            if slot == SLOT_FACTORS + 1:
+                factor_exps()
             head_at(slot, 1, regroup_v)
             unit_at(slot, LAG_JOIN, join)
             quad_at(slot, LAG_SQUARES, square_sums)
@@ -605,9 +603,12 @@ def tile_attention_pb_kernel(
             unit_at(slot, LAG_RESCALE, rescale)
             head_at(slot, 0, factor_gain)
             unit_at(slot, LAG_ENERGY, maxima)
+            if slot == SLOT_FACTORS:
+                factor_dots()
             if slot == SLOT_FACTORS + 1:
                 factor_bases()
                 factor_spread()
+            piece_at(slot, 0, flip_qk)
             quad_at(slot, LAG_WEIGH, weigh)
 
         nc.scalar.activation(out=warm[:], in_=eps[:], func=ACT.Sqrt)
@@ -621,8 +622,8 @@ def tile_attention_pb_kernel(
         join(30)
         join(31)
         early_rms()
-        for quad in range(5):
-            divide(quad)
+        divide(0, nc.vector)
+        divide(1, nc.vector)
         square_sums(5)
         regroup_scores(14)
         flip_scores(15)
@@ -630,13 +631,16 @@ def tile_attention_pb_kernel(
         regroup_scores(15)
         quantise_scores(13)
         multiply(13)
+        divide(2, nc.vector)
         quantise_scores(14)
         multiply(14)
+        divide(3, nc.vector)
         square_sums(6)
         square_sums(7)
         roots(6)
         quantise_scores(15)
         multiply(15)
+        divide(4, nc.vector)
         square_sums(8)
         finish(5)
         finish(6)

from contextlib import ExitStack

import concourse.mybir as mybir
from concourse.masks import make_identity

FP8X4 = mybir.dt.float8_e4m3fn_x4
BF16 = mybir.dt.bfloat16
F32 = mybir.dt.float32
U32 = mybir.dt.uint32
U8 = mybir.dt.uint8
ALU = mybir.AluOpType
ACT = mybir.ActivationFunctionType
AX = mybir.AxisListType

P = 128
S = 512
D = 1024
H = 8
HD = 128
C = 2
ROW_TILES = S // P
PACK = 4
D_PASSES = D // (PACK * P)
QUAD = 4
PAIR = 2
UNITS = ROW_TILES * H
PAIRS = UNITS // PAIR
GROUPS = [(2 * q, 2 * q + 1) for q in range(PAIRS // 2 - 1)] + [(PAIRS - 2,), (PAIRS - 1,)]
SM_SCALE = 1.0 / (HD ** 0.5)
EPS = 1e-9
MASKED = -1.0e30

LAG_ENERGY = -1
LAG_EXP = 0
LAG_RESCALE = 1
LAG_JOIN = 3
LAG_FLIP = 5
LAG_REGROUP = 6
LAG_QUANTISE = 8
LAG_MULTIPLY = 9
LAG_SQUARES = 1
LAG_WEIGH = 2
VALUE_PASSES = 6
SLOT_FACTORS = -1
SLOT_VALUE_PATH = 0
SLOT_PROJECT = 6
SLOT_VALUES = 14

FLOPS = 2 * S * D * H * HD + 2 * H * C * S * S * HD + 2 * H * S * S * HD


def tile_attention_pb_kernel(
    tc, q_rot, k_rot, h_norm, wv, head_norm_w, q1, q2, k1, k2, lam_init, out
):
    nc = tc.nc
    with ExitStack() as ctx:
        consts = ctx.enter_context(tc.tile_pool(name="consts", bufs=1))
        loads = ctx.enter_context(tc.tile_pool(name="loads", bufs=1))
        keep = ctx.enter_context(tc.tile_pool(name="keep", bufs=1))
        work = ctx.enter_context(tc.tile_pool(name="work", bufs=2))
        small = ctx.enter_context(tc.tile_pool(name="small", bufs=6))
        psum_e = ctx.enter_context(tc.psum_pool(name="psum_e", bufs=4))
        psum_t = ctx.enter_context(tc.psum_pool(name="psum_t", bufs=2))
        psum_att = ctx.enter_context(tc.psum_pool(name="psum_att", bufs=2))
        ctx.enter_context(tc.manual_schedule())

        neg_half = consts.tile([P, QUAD], F32, name="neg_half")
        nc.vector.memset(neg_half[:], -0.5)
        ident_bf = consts.tile([P, P], BF16, name="ident_bf")
        nc.vector.memset(ident_bf[:], 0.0)
        make_identity(nc, ident_bf[:], nomemset=True)
        row0 = consts.tile([P, 2 * P], BF16, name="row0")
        nc.vector.memset(row0[:], 0.0)

        q_rows = q_rot.rearrange("b s h m -> (b s) (h m)")
        k_rows = k_rot.rearrange("b s h m -> (b s) (h m)")
        q_sb = [loads.tile([P, H * C * HD], BF16, name="q_sb%d" % it) for it in range(ROW_TILES)]
        k_sb = [loads.tile([P, H * C * HD], BF16, name="k_sb%d" % it) for it in range(ROW_TILES)]

        def load_qk(it, cols):
            rows = slice(it * P, (it + 1) * P)
            nc.sync.dma_start(out=q_sb[it][:, cols], in_=q_rows[rows, cols])
            nc.sync.dma_start(out=k_sb[it][:, cols], in_=k_rows[rows, cols])

        quarter = H * C * HD // 4
        load_qk(0, slice(0, quarter))
        load_qk(0, slice(quarter, 2 * quarter))

        warm = consts.tile([P, 1], F32, name="warm")
        nc.scalar.activation(out=warm[:], in_=neg_half[:, 0:1], func=ACT.Exp)

        h_sb = loads.tile([P, ROW_TILES, D], BF16, name="h_sb")
        h_halves = h_sb[:].rearrange("p (u e) k -> p u (e k)", u=2)
        h_rows = h_norm.rearrange("b s k -> (b s) k").rearrange("(u p e) k -> p u (e k)", u=2, e=2)
        for u in range(2):
            nc.sync.dma_start(out=h_halves[:, u, :], in_=h_rows[:, u, :])
        qk_vec = consts.tile([H, 4, HD], BF16, name="qk_vec")
        for n, vec in enumerate((q1, q2, k1, k2)):
            nc.scalar.dma_start(out=qk_vec[:, n, :], in_=vec.rearrange("h d o -> h (d o)"))
        nc.scalar.dma_start(out=row0[0:1, 0:HD], in_=head_norm_w.rearrange("(o d) -> o d", o=1))
        nc.scalar.dma_start(out=row0[0:1, P : P + H], in_=lam_init.rearrange("(o h) -> o h", o=1))
        load_qk(0, slice(2 * quarter, 4 * quarter))
        w_sb = loads.tile([P, H, D], BF16, name="w_sb")
        w_tiles = wv.rearrange("(o p) k -> p o k", p=P)

        def load_w(half):
            for first in range(half * QUAD, (half + 1) * QUAD, PAIR):
                heads = slice(first, first + PAIR)
                nc.sync.dma_start(out=w_sb[:, heads, :], in_=w_tiles[:, heads, :])

        load_w(0)
        load_w(1)
        load_qk(1, slice(0, 4 * quarter))
        for it in range(2, ROW_TILES):
            load_qk(it, slice(0, 4 * quarter))

        mask_f32 = consts.tile([P, P], F32, name="mask_f32")
        nc.vector.memset(mask_f32[:], 0.0)
        nc.gpsimd.affine_select(
            out=mask_f32[:],
            in_=mask_f32[:],
            compare_op=ALU.is_ge,
            fill=MASKED,
            base=0,
            pattern=[[-1, P]],
            channel_multiplier=1,
        )
        ident_f32 = consts.tile([P, P], F32, name="ident_f32")
        nc.vector.memset(ident_f32[:], 0.0)
        make_identity(nc, ident_f32[:], nomemset=True)
        ones_bf = consts.tile([P, P], BF16, name="ones_bf")
        nc.vector.memset(ones_bf[:], 1.0)
        eps = consts.tile([P, 1], F32, name="eps")
        nc.vector.memset(eps[:], EPS)
        base = consts.tile([P, 1], F32, name="base")
        nc.vector.memset(base[:], 0.0)
        sc_sb = keep.tile([P, H, S], BF16, name="sc_sb")
        nc.vector.memset(sc_sb[:].rearrange("p h s -> p (h s)").bitcast(U32), 0)
        mask_bf = consts.tile([P, P], BF16, name="mask_bf")
        nc.vector.tensor_copy(out=mask_bf[:], in_=mask_f32[:])

        scale_all = consts.tile([P, H], F32, name="scale_all")
        gain = consts.tile([P, H, HD], F32, name="gain")

        dots = consts.tile([H, 2], F32, name="dots")
        exps = consts.tile([H, 2], F32, name="exps")
        one_minus_lam = consts.tile([P, H], F32, name="one_minus_lam")
        row_all = consts.tile([P, P + H], F32, name="row_all")
        w_all = row_all[:, 0:HD]
        lam_all = row_all[:, P : P + H]
        factor_banks = {}

        def factor_dots():
            prod = consts.tile([H, 2, HD], F32, name="prod")
            nc.vector.tensor_tensor(out=prod[:], in0=qk_vec[:, 0:2, :], in1=qk_vec[:, 2:4, :], op=ALU.mult)
            nc.vector.reduce_sum(out=dots[:], in_=prod[:], axis=AX.X)

        def factor_exps():
            nc.scalar.activation(out=exps[:], in_=dots[:], func=ACT.Exp)

        def factor_bases():
            nc.vector.tensor_sub(out=base[0:H, :], in0=exps[:, 0:1], in1=exps[:, 1:2])

        def factor_spread():
            bank = psum_e.tile([P, 3, P], F32, name="factor_bank", tag="e")
            base_all, row_bank = bank[:, 0, :], bank[:, 1:3, :].rearrange("p a c -> p (a c)")
            nc.tensor.matmul(
                base_all, lhsT=base[:, 0:1].to_broadcast([P, P]), rhs=ident_f32[:], start=True, stop=True
            )
            nc.tensor.matmul(row_bank, lhsT=ones_bf[:], rhs=row0[:], start=True, stop=True)
            factor_banks["base"] = base_all
            factor_banks["row"] = row_bank

        def factor_scales():
            nc.vector.tensor_copy(out=row_all[:], in_=factor_banks["row"][:, 0 : P + H])
            lam_sum = consts.tile([P, 1], F32, name="lam_sum")
            nc.vector.reduce_sum(out=lam_sum[:], in_=lam_all, axis=AX.X)
            nc.vector.tensor_scalar(
                out=scale_all[:],
                in0=factor_banks["base"][:, 0:H],
                scalar1=-float(H),
                scalar2=lam_sum[:, 0:1],
                op0=ALU.mult,
                op1=ALU.subtract,
            )

        def factor_gain(h):
            if h == 0:
                nc.gpsimd.tensor_scalar(
                    out=one_minus_lam[:], in0=lam_all, scalar1=-1.0, scalar2=1.0, op0=ALU.mult, op1=ALU.add
                )
            nc.gpsimd.tensor_scalar(
                out=gain[:, h, :],
                in0=w_all,
                scalar1=one_minus_lam[:, h : h + 1],
                scalar2=0.0,
                op0=ALU.mult,
                op1=ALU.add,
            )

        qT = keep.tile([P, H * C, S], BF16, name="qT")
        kT = keep.tile([P, H * C, S], BF16, name="kT")

        def qk_piece(which, it, first, heads):
            return (q_sb, k_sb)[which][it], (qT, kT)[which], it, first * C, heads * C

        pieces = [
            (-2, qk_piece(0, 0, 0, 2)),
            (-2, qk_piece(1, 0, 0, 2)),
            (-1, qk_piece(0, 0, 2, 2)),
            (-1, qk_piece(1, 0, 2, 2)),
            (0, qk_piece(0, 0, 4, 4)),
            (1, qk_piece(1, 0, 4, 4)),
        ]
        for it in range(1, ROW_TILES):
            for n in range(4):
                pieces.append(((it - 1) * H + ((4, 5, 6, 8) if it == 1 else (2, 4, 6, 8))[n], qk_piece(n % 2, it, n // 2 * 4, 4)))
        qk_banks = {}

        def flip_qk(piece):
            rows_sb, flipped, it, first, count = pieces[piece][1]
            bank = psum_t.tile([P, count, P], BF16, name="qk_bank", tag="t")
            for n in range(count):
                hc = first + n
                nc.tensor.transpose(bank[:, n, :], rows_sb[:, hc * HD : (hc + 1) * HD], ident_bf[:])
            qk_banks[piece] = bank

        def keep_qk(piece, on_vector=False):
            rows_sb, flipped, it, first, count = pieces[piece][1]
            kept = flipped[:, first : first + count, it * P : (it + 1) * P]
            bank = qk_banks.pop(piece)
            if on_vector:
                nc.vector.tensor_copy(out=kept, in_=bank[:])
            else:
                nc.scalar.copy(out=kept, in_=bank[:])

        def word_transposes(bank, pair_words):
            for r in range(2):
                for u in range(2):
                    nc.tensor.transpose(bank[:, r, u, :], pair_words[r][:, u * P : (u + 1) * P], ident_f32[:])

        def flip_512_rows(rows_words, g):
            banks = []
            for half in range(2):
                bank = psum_att.tile([P, 2, 2, P], F32, name="kl_bank", tag="att")
                word_transposes(
                    bank, [rows_words[:, 2 * half + r, g * 2 * P : (g + 1) * 2 * P] for r in range(2)]
                )
                banks.append(bank)
            return banks

        def regroup_512_rows(banks):
            grouped = work.tile([P, QUAD * P, PACK], BF16, name="grouped", bufs=3, align_bytes=64)
            halves = grouped[:].bitcast(F32).rearrange("p (a r c) u -> p a r c u", a=2, r=2)
            nc.vector.tensor_copy(out=halves[:, 0], in_=banks[0][:].rearrange("p r u c -> p r c u"))
            nc.scalar.copy(out=halves[:, 1], in_=banks[1][:].rearrange("p r u c -> p r c u"))
            return grouped

        h_codes = keep.tile([P, D_PASSES, S], U32, name="h_codes", align_bytes=64)
        h_scales = keep.tile([P, D_PASSES, S], U8, name="h_scales", align_bytes=64)
        w_codes = keep.tile([P, D_PASSES, H * HD], U32, name="w_codes", align_bytes=64)
        w_scales = keep.tile([P, D_PASSES, H * HD], U8, name="w_scales", align_bytes=64)
        v_grouped = keep.tile([P, H, HD, PACK], BF16, name="v_grouped", align_bytes=64)
        v_codes = keep.tile([P, H * HD], U32, name="v_codes", align_bytes=64)
        v_scales = keep.tile([P, H * HD], U8, name="v_scales", align_bytes=64)

        def quantise_512_rows(grouped, codes, scales):
            nc.vector.quantize_mx(
                out=codes.bitcast(FP8X4), scales=scales, in_=grouped[:].rearrange("p c t -> p (c t)")
            )

        v_banks = {}

        def project(h):
            d_cols = slice(h * HD, (h + 1) * HD)
            v_bank = psum_att.tile([P, ROW_TILES, HD], F32, name="v_bank", tag="att")
            for t in range(ROW_TILES):
                j_cols = slice(t * P, (t + 1) * P)
                for g in range(D_PASSES):
                    nc.tensor.matmul_mx(
                        out=v_bank[:, t, :],
                        lhsT=h_codes[:, g, j_cols].bitcast(FP8X4),
                        lhsT_scale=h_scales[:, g, j_cols],
                        rhs=w_codes[:, g, d_cols].bitcast(FP8X4),
                        rhs_scale=w_scales[:, g, d_cols],
                        start=(g == 0),
                        stop=(g == D_PASSES - 1),
                    )
            v_banks[h] = v_bank

        def regroup_v(h):
            v_bank = v_banks.pop(h)
            if h % 2 >= 0:
                nc.vector.tensor_copy(out=v_grouped[:, h, :, :], in_=v_bank[:].rearrange("p t d -> p d t"))
            else:
                nc.scalar.copy(out=v_grouped[:, h, :, :], in_=v_bank[:].rearrange("p t d -> p d t"))

        def quantise_v(half):
            cols = slice(half * QUAD * HD, (half + 1) * QUAD * HD)
            nc.vector.quantize_mx(
                out=v_codes[:, cols].bitcast(FP8X4),
                scales=v_scales[:, cols],
                in_=v_grouped[:, half * QUAD : (half + 1) * QUAD, :, :].rearrange("p a d t -> p (a d t)"),
            )

        unit_tiles = {}

        def energies(k):
            it, h = divmod(k, H)
            n = (it + 1) * P
            rows = slice(it * P, n)
            if C * n <= S:
                both = psum_e.tile([P, C, n], F32, name="e", tag="e")
                energy = [both[:, c, :] for c in range(C)]
                banks = [both[:]]
            else:
                energy = [psum_e.tile([P, n], F32, name="e", tag="e")[:] for c in range(C)]
                banks = energy
            for c in range(C):
                hc = h * C + c
                nc.tensor.matmul(energy[c], lhsT=qT[:, hc, rows], rhs=kT[:, hc, :n], start=True, stop=False)
                nc.tensor.matmul(energy[c][:, rows], lhsT=ident_bf[:], rhs=mask_bf[:], start=False, stop=True)
            unit_tiles[k] = {"energy": energy, "banks": banks}

        def maxima(k):
            top = small.tile([P, C], F32, name="top")
            banks = unit_tiles[k]["banks"]
            per_bank = C // len(banks)
            for n, bank in enumerate(banks):
                nc.vector.reduce_max(out=top[:, n * per_bank : (n + 1) * per_bank], in_=bank, axis=AX.X)
            unit_tiles[k]["top"] = top

        def shifts(k):
            shift = small.tile([P, C], F32, name="shift")
            nc.scalar.activation(out=shift[:], in_=unit_tiles[k]["top"][:], func=ACT.Copy, scale=-SM_SCALE)
            unit_tiles[k]["shift"] = shift

        def exponentials(k):
            n = (k // H + 1) * P
            sums = small.tile([P, C], F32, name="sums")
            probs = []
            for c in range(C):
                p = work.tile([P, S], F32, name="p%d" % c, bufs=5)
                nc.scalar.activation(
                    out=p[:, :n],
                    in_=unit_tiles[k]["energy"][c],
                    func=ACT.Exp,
                    bias=unit_tiles[k]["shift"][:, c : c + 1],
                    scale=SM_SCALE,
                    accum_out=sums[:, c : c + 1],
                )
                probs.append(p)
            unit_tiles[k]["sums"] = sums
            unit_tiles[k]["probs"] = probs

        def rescale(k):
            it, h = divmod(k, H)
            n = (it + 1) * P
            recip = small.tile([P, C], F32, name="recip")
            nc.vector.reciprocal(out=recip[:], in_=unit_tiles[k]["sums"][:])
            p1 = unit_tiles[k]["probs"][1]
            engine = nc.vector if k >= UNITS - PAIR else nc.gpsimd
            engine.tensor_scalar(
                out=p1[:, :n],
                in0=p1[:, :n],
                scalar1=recip[:, 1:2],
                scalar2=scale_all[:, h : h + 1],
                op0=ALU.mult,
                op1=ALU.mult,
            )
            unit_tiles[k]["recip"] = recip

        def join(k):
            it, h = divmod(k, H)
            n = (it + 1) * P
            tiles = unit_tiles.pop(k)
            nc.vector.scalar_tensor_tensor(
                out=sc_sb[:, h, :n],
                in0=tiles["probs"][0][:, :n],
                scalar=tiles["recip"][:, 0:1],
                in1=tiles["probs"][1][:, :n],
                op0=ALU.mult,
                op1=ALU.add,
            )

        pair_tiles = {}
        quad_tiles = {}
        sum_all = keep.tile([P, 5 * QUAD], F32, name="sum_all")
        root_all = keep.tile([P, 5 * QUAD], F32, name="root_all")
        rstd_all = keep.tile([P, 5 * QUAD], F32, name="rstd_all")
        weighed = keep.tile([P, 5 * QUAD, HD], F32, name="weighed")
        late_quads = range(len(GROUPS) - 4, len(GROUPS))
        group_of = {m: g for g, pairs in enumerate(GROUPS) for m in pairs}
        out_rows = out.rearrange("b s h d -> (b s) (h d)")

        def flip_scores(m):
            first = (m * PAIR) % H
            bank = psum_t.tile([P, PAIR, 2, P], F32, name="sc_bank", tag="t")
            word_transposes(bank, [sc_sb[:, first + r, :].bitcast(F32) for r in range(PAIR)])
            pair_tiles[m] = {"bank": bank}

        def regroup_scores(m):
            sc_grouped = work.tile([P, PAIR, P, PACK], BF16, name="sc_grouped", align_bytes=64)
            nc.scalar.copy(
                out=sc_grouped[:].bitcast(F32), in_=pair_tiles[m]["bank"][:].rearrange("p r u c -> p r c u")
            )
            pair_tiles[m]["grouped"] = sc_grouped

        def quantise_scores(m):
            sc_codes = work.tile([P, PAIR * P], U32, name="sc_codes", bufs=6, align_bytes=64)
            sc_scales = work.tile([P, PAIR * P], U8, name="sc_scales", bufs=6, align_bytes=64)
            nc.vector.quantize_mx(
                out=sc_codes[:].bitcast(FP8X4),
                scales=sc_scales[:],
                in_=pair_tiles[m]["grouped"][:].rearrange("p r c t -> p (r c t)"),
            )
            pair_tiles[m]["codes"] = sc_codes
            pair_tiles[m]["scales"] = sc_scales

        def multiply(m):
            first = (m * PAIR) % H
            quad = group_of[m]
            second = GROUPS[quad].index(m)
            if not second:
                pool, tag = (psum_e, "e") if m >= PAIRS - 2 else (psum_att, "att")
                quad_tiles[quad] = {"att": pool.tile([P, QUAD, HD], F32, name="att", tag=tag)}
            tiles = pair_tiles.pop(m)
            for r in range(PAIR):
                i_cols = slice(r * P, (r + 1) * P)
                d_cols = slice((first + r) * HD, (first + r + 1) * HD)
                nc.tensor.matmul_mx(
                    out=quad_tiles[quad]["att"][:, second * PAIR + r, :],
                    lhsT=tiles["codes"][:, i_cols].bitcast(FP8X4),
                    lhsT_scale=tiles["scales"][:, i_cols],
                    rhs=v_codes[:, d_cols].bitcast(FP8X4),
                    rhs_scale=v_scales[:, d_cols],
                    start=True,
                    stop=True,
                )

        def square_sums(quad):
            squares = work.tile([P, QUAD, HD], BF16, name="squares")
            heads = PAIR * len(GROUPS[quad])
            if quad in late_quads:
                sum_sq = small.tile([P, QUAD], F32, name="sum_sq")
            else:
                sum_sq = sum_all[:, quad * QUAD : (quad + 1) * QUAD]
            for r in range(heads):
                nc.scalar.activation(
                    out=squares[:, r, :],
                    in_=quad_tiles[quad]["att"][:, r, :],
                    func=ACT.Square,
                    accum_out=sum_sq[:, r : r + 1],
                )
            quad_tiles[quad]["sum_sq"] = sum_sq[:, 0:heads]

        def weigh(quad):
            it, first = divmod(quad * QUAD, H)
            nc.vector.tensor_tensor(
                out=weighed[:, quad * QUAD : (quad + 1) * QUAD, :],
                in0=quad_tiles.pop(quad)["att"][:],
                in1=gain[:, first : first + QUAD, :],
                op=ALU.mult,
            )

        def roots(quad):
            root = small.tile([P, QUAD], F32, name="root")
            heads = PAIR * len(GROUPS[quad])
            nc.scalar.activation(
                out=root[:, 0:heads], in_=quad_tiles[quad]["sum_sq"], func=ACT.Sqrt, bias=eps[:, 0:1], scale=1.0 / HD
            )
            quad_tiles[quad]["root"] = root

        def early_roots():
            nc.scalar.activation(out=root_all[:], in_=sum_all[:], func=ACT.Sqrt, bias=eps[:, 0:1], scale=1.0 / HD)

        def early_rms():
            nc.vector.reciprocal(out=rstd_all[:], in_=root_all[:])

        def divide(quad, engine=nc.gpsimd):
            it, first = divmod(quad * QUAD, H)
            rows = weighed[:, quad * QUAD : (quad + 1) * QUAD, :]
            for r in range(QUAD):
                n = quad * QUAD + r
                engine.tensor_scalar(
                    out=weighed[:, n, :],
                    in0=weighed[:, n, :],
                    scalar1=rstd_all[:, n : n + 1],
                    scalar2=0.0,
                    op0=ALU.mult,
                    op1=ALU.add,
                )
            nc.sync.dma_start(
                out=out_rows[it * P : (it + 1) * P, first * HD : (first + QUAD) * HD],
                in_=rows.rearrange("p r d -> p (r d)"),
            )

        def finish(quad):
            it, first = divmod(GROUPS[quad][0] * PAIR, H)
            heads = PAIR * len(GROUPS[quad])
            tiles = quad_tiles.pop(quad)
            normed = work.tile([P, QUAD, HD], F32, name="normed", bufs=4)
            rstd = small.tile([P, QUAD], F32, name="rstd")
            nc.vector.reciprocal(out=rstd[:, 0:heads], in_=tiles["root"][:, 0:heads])
            for r in range(heads):
                nc.vector.scalar_tensor_tensor(
                    out=normed[:, r, :],
                    in0=tiles["att"][:, r, :],
                    scalar=rstd[:, r : r + 1],
                    in1=gain[:, first + r, :],
                    op0=ALU.mult,
                    op1=ALU.mult,
                )
            nc.sync.dma_start(
                out=out_rows[it * P : (it + 1) * P, first * HD : (first + heads) * HD],
                in_=normed[:, 0:heads, :].rearrange("p r d -> p (r d)"),
            )

        def unit_at(slot, lag, stage):
            k = slot - lag
            if 0 <= k < UNITS:
                stage(k)

        def pair_at(slot, lag, stage):
            m, odd = divmod(slot - lag, PAIR)
            if odd == 0 and 0 <= m < PAIRS:
                stage(m)

        def multiply_slot(m):
            return max(2 * m + LAG_MULTIPLY, SLOT_VALUES + m + (m >= QUAD))

        def quad_at(slot, lag, stage):
            for quad in range(len(GROUPS)):
                if multiply_slot(GROUPS[quad][-1]) + lag == slot:
                    stage(quad)

        def piece_at(slot, lag, stage):
            for piece in range(len(pieces)):
                if pieces[piece][0] + lag == slot:
                    stage(piece)

        value_passes = []
        for rows_sb, codes, scales in (
            (h_sb[:], h_codes[:], h_scales[:]),
            (w_sb[:, 0:QUAD, :], w_codes[:, :, 0:S], w_scales[:, :, 0:S]),
            (w_sb[:, QUAD:H, :], w_codes[:, :, S : 2 * S], w_scales[:, :, S : 2 * S]),
        ):
            for g in range(D_PASSES):
                value_passes.append((rows_sb.bitcast(F32), g, codes[:, g, :], scales[:, g, :]))
        value_tiles = {}

        def flip_value(n):
            rows_words, g, codes, scales = value_passes[n]
            value_tiles[n] = flip_512_rows(rows_words, g)

        def regroup_value(n):
            value_tiles[n] = regroup_512_rows(value_tiles[n])

        def quantise_value(n):
            rows_words, g, codes, scales = value_passes[n]
            quantise_512_rows(value_tiles.pop(n), codes, scales)

        def pass_at(slot, lag, stage):
            if 0 <= slot - lag < VALUE_PASSES:
                stage(slot - lag)

        def head_at(slot, lag, stage):
            h = slot - SLOT_PROJECT - lag
            if 0 <= h < H:
                stage(h)

        flip_qk(0)
        flip_qk(1)
        keep_qk(0, on_vector=True)
        keep_qk(1)

        for slot in range(LAG_ENERGY, UNITS):
            unit_at(slot, LAG_ENERGY, energies)
            pair_at(slot, LAG_FLIP, flip_scores)
            head_at(slot, 0, project)
            for m in range(PAIRS):
                if multiply_slot(m) == slot:
                    multiply(m)
            pass_at(slot, SLOT_VALUE_PATH, flip_value)
            unit_at(slot, LAG_EXP, shifts)
            pass_at(slot, SLOT_VALUE_PATH + 1, regroup_value)
            if slot > LAG_ENERGY:
                piece_at(slot, 1, keep_qk)
            pair_at(slot, LAG_REGROUP, regroup_scores)
            unit_at(slot, LAG_EXP, exponentials)
            if slot == SLOT_FACTORS + 1:
                factor_exps()
            head_at(slot, 1, regroup_v)
            unit_at(slot, LAG_JOIN, join)
            quad_at(slot, LAG_SQUARES, square_sums)
            pass_at(slot, SLOT_VALUE_PATH + 2, quantise_value)
            for half in range(H // QUAD):
                if slot == SLOT_PROJECT + 1 + (half + 1) * QUAD:
                    quantise_v(half)
            pair_at(slot, LAG_QUANTISE, quantise_scores)
            if slot == SLOT_FACTORS + 2:
                factor_scales()
            unit_at(slot, LAG_RESCALE, rescale)
            head_at(slot, 0, factor_gain)
            unit_at(slot, LAG_ENERGY, maxima)
            if slot == SLOT_FACTORS:
                factor_dots()
            if slot == SLOT_FACTORS + 1:
                factor_bases()
                factor_spread()
            piece_at(slot, 0, flip_qk)
            quad_at(slot, LAG_WEIGH, weigh)

        nc.scalar.activation(out=warm[:], in_=eps[:], func=ACT.Sqrt)
        early_roots()
        quantise_scores(12)
        join(29)
        multiply(12)
        flip_scores(14)
        rescale(31)
        regroup_scores(13)
        join(30)
        join(31)
        early_rms()
        divide(0, nc.vector)
        divide(1, nc.vector)
        square_sums(5)
        regroup_scores(14)
        flip_scores(15)
        roots(5)
        regroup_scores(15)
        quantise_scores(13)
        multiply(13)
        divide(2, nc.vector)
        quantise_scores(14)
        multiply(14)
        divide(3, nc.vector)
        square_sums(6)
        square_sums(7)
        roots(6)
        quantise_scores(15)
        multiply(15)
        divide(4, nc.vector)
        square_sums(8)
        finish(5)
        finish(6)
        roots(7)
        roots(8)
        finish(7)
        finish(8)
